import numpy as np
import ml_dtypes


def mxq(x, axis, fmt="e4m3"):
    dtype, down = {"e4m3": (ml_dtypes.float8_e4m3fn, 7), "e5m2": (ml_dtypes.float8_e5m2, 14)}[fmt]
    v = np.moveaxis(np.asarray(x, np.float32).astype(ml_dtypes.bfloat16).astype(np.float64), axis, -1)
    blocks = v.reshape(v.shape[:-1] + (-1, 32))
    amax = np.abs(blocks).max(-1, keepdims=True)
    byte = np.maximum(np.where(amax > 0, np.frexp(amax)[1] - 1 + 127, 0) - down, 1)
    scale = np.exp2(byte - 127.0)
    codes = (blocks / scale).astype(np.float32).astype(dtype).astype(np.float64)
    return np.moveaxis((codes * scale).reshape(v.shape), -1, axis)


WIDE = False


def mx_kscale(k):
    if not WIDE:
        return np.ones(k)
    levels = np.array([10, -10, 5, -5, 0])
    a = np.random.permutation(np.resize(levels, k // 512 * 4)).reshape(k // 512, 4)
    idx = np.arange(k)
    return np.exp2(a[idx // 512, idx % 128 // 32])


BF16 = ml_dtypes.bfloat16


def bf(x):
    return np.asarray(x, np.float32).astype(BF16)


def f64(x):
    return np.asarray(x).astype(np.float64)


E2M1 = np.array([0.0, 0.5, 1.0, 1.5, 2.0, 3.0, 4.0, 6.0, -0.0, -0.5, -1.0, -1.5, -2.0, -3.0, -4.0, -6.0])


def pack_weight(w, fmt):
    k, n = w.shape
    w = f64(bf(w)).reshape(k // 32, 32, n)
    amax = np.abs(w).max(1)
    if fmt == "e4m3":
        byte = np.frexp(amax)[1] - 1 + 127 - 7
    else:
        mant, ex = np.frexp(amax / 6.0)
        byte = np.where(mant > 0.5, ex, ex - 1) + 127
    byte = np.clip(np.where(amax > 0, byte, 1), 1, 254)
    scaled = (w * np.exp2(127.0 - byte)[:, None, :]).reshape(k, n).astype(np.float32)
    by_word = np.ascontiguousarray(scaled.reshape(k // 512, 128, 4, n).transpose(0, 1, 3, 2))
    if fmt == "e4m3":
        words = by_word.astype(ml_dtypes.float8_e4m3fn).view(np.uint8)
    else:
        c = by_word.astype(ml_dtypes.float4_e2m1fn).view(np.uint8) & 0xF
        words = c[..., 0::2] | (c[..., 1::2] << 4)
    return np.ascontiguousarray(words), np.ascontiguousarray(byte.astype(np.uint8).reshape(k // 512, 16, n))


def unpack_weight(words, scales, fmt):
    g, p, n, _ = words.shape
    if fmt == "e4m3":
        vals = np.ascontiguousarray(words).view(ml_dtypes.float8_e4m3fn).astype(np.float64)
    else:
        nib = np.empty((g, p, n, 4), np.uint8)
        nib[..., 0::2] = words & 0xF
        nib[..., 1::2] = words >> 4
        vals = E2M1[nib]
    vals = vals * np.repeat(np.exp2(scales.astype(np.float64) - 127.0), 8, axis=1)[..., None]
    return vals.transpose(0, 1, 3, 2).reshape(g * 512, n)


E, T, H, D, R = 4, 256, 1024, 1024, 128
SCALE = 2.0
FMT = "e4m3"


def silu(v):
    return v / (1.0 + np.exp(-v))


def setup_inputs():
    s = mx_kscale(H)
    x = bf(np.random.standard_normal((E, T, H)) * s)
    low_gu = bf(np.random.standard_normal((E, T, R)))
    W_gu = np.random.standard_normal((E, 2 * D, H)) / np.sqrt(H) / s
    B_gu = bf(np.random.standard_normal((E, 2 * D, R)) * 0.3 / np.sqrt(R))
    A_d = np.random.standard_normal((E, R, D)) * 1.5 / np.sqrt(D)
    W_gu_words, W_gu_scales = pack_weight(np.ascontiguousarray(W_gu.swapaxes(1, 2)).reshape(-1, 2 * D), FMT)
    A_d_words, A_d_scales = pack_weight(np.ascontiguousarray(A_d.swapaxes(1, 2)).reshape(-1, R), FMT)
    return {"x": x,
            "low_gu": low_gu,
            "W_gu_words": W_gu_words,
            "W_gu_scales": W_gu_scales,
            "B_gu": B_gu,
            "A_d_words": A_d_words,
            "A_d_scales": A_d_scales}


def reference(x, low_gu, W_gu_words, W_gu_scales, B_gu, A_d_words, A_d_scales):
    base = mxq(f64(x), 2, "e4m3") @ unpack_weight(W_gu_words, W_gu_scales, FMT).reshape(E, H, 2 * D)
    delta = f64(low_gu) @ f64(B_gu).transpose(0, 2, 1)
    gate_up = base + SCALE * delta
    gate, up = gate_up[..., :D], gate_up[..., D:]
    h = up * silu(gate)
    low_d = mxq(h, 2, "e4m3") @ unpack_weight(A_d_words, A_d_scales, FMT).reshape(E, D, R)
    return h, low_d

@@ -1,0 +1,256 @@
+from contextlib import ExitStack
+
+import concourse.mybir as mybir
+from concourse.masks import make_identity
+
+F32 = mybir.dt.float32
+BF16 = mybir.dt.bfloat16
+I32 = mybir.dt.int32
+U32 = mybir.dt.uint32
+U8 = mybir.dt.uint8
+FP8X4 = mybir.dt.float8_e4m3fn_x4
+ALU = mybir.AluOpType
+ACT = mybir.ActivationFunctionType
+
+E, T, H, D, R = 4, 256, 1024, 1024, 128
+P = 128
+PACK = 4
+K_PASS = P * PACK
+BANK = 512
+TOKEN_TILES = T // P
+H_PASSES = H // K_PASS
+D_PASSES = D // K_PASS
+N_BANKS = 2 * D // BANK
+PLANES_PER_TILE = 4
+LORA_SCALE = 2.0
+
+FLOPS = 2 * E * T * (2 * D) * H + 2 * E * T * (2 * D) * R + 2 * E * T * D * R
+
+
+def tile_loralinearexpertswrapper_pa_e_kernel(
+    tc, x, low_gu, W_gu_words, W_gu_scales, B_gu, A_d_words, A_d_scales, out_0, out_1
+):
+    nc = tc.nc
+    with ExitStack() as ctx:
+        keep = ctx.enter_context(tc.tile_pool(name="keep", bufs=1))
+        work = ctx.enter_context(tc.tile_pool(name="work", bufs=2))
+        psum = ctx.enter_context(tc.psum_pool(name="psum", bufs=2))
+
+        x_sb = [keep.tile([P, TOKEN_TILES, H], BF16, name="x_sb%d" % e) for e in range(E)]
+        low_sb = keep.tile([P, E, TOKEN_TILES, R], BF16, name="low_sb")
+        b_sb = [keep.tile([P, N_BANKS, PACK, R], BF16, name="b_sb%d" % e) for e in range(E)]
+        w_words = [
+            keep.tile([P, 2 * D], U32, name="w_words%d" % g, align_bytes=64) for g in range(E * H_PASSES)
+        ]
+        w_planes = [
+            keep.tile([P, 2 * D], U8, name="w_planes%d" % b, align_bytes=64)
+            for b in range(E * H_PASSES // PLANES_PER_TILE)
+        ]
+        a_words = keep.tile([P, E * D_PASSES, R], U32, name="a_words", align_bytes=64)
+        a_planes = keep.tile([P, E * D_PASSES, R], U8, name="a_planes", align_bytes=64)
+
+        for plane_tile in w_planes:
+            nc.vector.memset(plane_tile[:].bitcast(I32), 0)
+        nc.vector.memset(a_planes[:].rearrange("p g n -> p (g n)").bitcast(I32), 0)
+
+        ident_bf16 = keep.tile([P, P], BF16, name="ident_bf16")
+        make_identity(nc, ident_bf16[:])
+        ident_f32 = keep.tile([P, P], F32, name="ident_f32")
+        make_identity(nc, ident_f32[:])
+
+        def load_tokens(e):
+            nc.sync.dma_start(out=x_sb[e][:], in_=x[e].rearrange("(p m) k -> p m k", m=TOKEN_TILES))
+            nc.sync.dma_start(
+                out=b_sb[e][:],
+                in_=B_gu[e].rearrange("(q p j) r -> p q j r", q=N_BANKS, p=P, j=PACK),
+            )
+
+        def load_w_planes(b):
+            for quadrant in range(4):
+                nc.sync.dma_start(
+                    out=w_planes[b][32 * quadrant : 32 * quadrant + 16, :].bitcast(I32),
+                    in_=W_gu_scales[
+                        PLANES_PER_TILE * b : PLANES_PER_TILE * (b + 1), 4 * quadrant : 4 * quadrant + 4, :
+                    ].bitcast(I32),
+                )
+
+        def load_a_planes():
+            for quadrant in range(4):
+                nc.sync.dma_start(
+                    out=a_planes[32 * quadrant : 32 * quadrant + 4, :, :].bitcast(I32),
+                    in_=A_d_scales[:, 4 * quadrant : 4 * quadrant + 4, :].rearrange("g r n -> r g n").bitcast(I32),
+                )
+
+        def load_w_words(e):
+            for kc in range(H_PASSES):
+                g = H_PASSES * e + kc
+                nc.sync.dma_start(
+                    out=w_words[g][:].bitcast(I32),
+                    in_=W_gu_words[g].rearrange("p n t -> p (n t)").bitcast(I32),
+                )
+
+        load_tokens(0)
+        nc.sync.dma_start(out=low_sb[:], in_=low_gu.rearrange("e (p m) r -> p e m r", m=TOKEN_TILES))
+        load_w_planes(0)
+        load_w_planes(1)
+        load_a_planes()
+        load_tokens(1)
+        load_w_words(0)
+        nc.sync.dma_start(
+            out=a_words[:].bitcast(I32), in_=A_d_words.rearrange("g p n t -> p g (n t)").bitcast(I32)
+        )
+        load_tokens(2)
+        load_w_words(1)
+        load_tokens(3)
+        load_w_words(2)
+        load_w_words(3)
+
+        low_t = keep.tile([P, E, TOKEN_TILES, P], BF16, name="low_t")
+        low_ps = psum.tile([P, E, TOKEN_TILES, P], BF16, tag="tr")
+        for e in range(E):
+            for m in range(TOKEN_TILES):
+                nc.tensor.transpose(low_ps[:, e, m, :], low_sb[:, e, m, :], ident_bf16[:])
+        nc.vector.tensor_copy(out=low_t[:], in_=low_ps[:])
+
+        x_words = {}
+        x_planes = {}
+        delta2 = {}
+
+        def prepare(e):
+            x_pairs = x_sb[e][:].rearrange("p m k -> p (m k)").bitcast(F32)
+            x_grouped = work.tile([P, H_PASSES, TOKEN_TILES, P, PACK], BF16, tag="x_grouped", align_bytes=64)
+            for kc in range(H_PASSES):
+                x_ps = psum.tile([P, TOKEN_TILES, 2, P], F32, tag="tr")
+                for m in range(TOKEN_TILES):
+                    for u in range(2):
+                        first = (H // 2) * m + (K_PASS // 2) * kc
+                        nc.tensor.transpose(
+                            x_ps[:, m, u, :], x_pairs[:, first + u : first + K_PASS // 2 : 2], ident_f32[:]
+                        )
+                nc.vector.tensor_copy(
+                    out=x_grouped[:, kc]
+                    .rearrange("p m r t -> p (m r t)")
+                    .bitcast(F32)
+                    .rearrange("p (m r u) -> p m r u", m=TOKEN_TILES, u=2),
+                    in_=x_ps[:].rearrange("p m u r -> p m r u"),
+                )
+            words = work.tile([P, H_PASSES, TOKEN_TILES, P], U32, tag="x_words", bufs=3, align_bytes=64)
+            planes = work.tile([P, H_PASSES, TOKEN_TILES, P], U8, tag="x_planes", bufs=3, align_bytes=64)
+            x_words[e] = words
+            x_planes[e] = planes
+
+            b_t = work.tile([P, N_BANKS, PACK * P], BF16, tag="b_t")
+            for half in range(2):
+                b_ps = psum.tile([P, 2, PACK, P], BF16, tag="tr")
+                for i in range(2):
+                    for j in range(PACK):
+                        nc.tensor.transpose(b_ps[:, i, j, :], b_sb[e][:, 2 * half + i, j, :], ident_bf16[:])
+                nc.scalar.copy(
+                    out=b_t[:, 2 * half : 2 * half + 2, :], in_=b_ps[:].rearrange("r i j p -> r i (j p)")
+                )
+
+            nc.vector.quantize_mx(
+                out=x_words[e][:].rearrange("p c m r -> p (c m r)").bitcast(FP8X4),
+                scales=x_planes[e][:].rearrange("p c m r -> p (c m r)"),
+                in_=x_grouped[:].rearrange("p c m r t -> p (c m r t)"),
+            )
+
+            doubled = work.tile([P, TOKEN_TILES, N_BANKS, BANK], F32, tag="delta2", bufs=3)
+            delta2[e] = doubled
+            for m in range(TOKEN_TILES):
+                for q in range(N_BANKS):
+                    delta_ps = psum.tile([P, BANK], F32, tag="delta")
+                    nc.tensor.matmul(delta_ps[:], lhsT=low_t[:, e, m, :], rhs=b_t[:, q, :], start=True, stop=True)
+                    ordered = delta2[e][:, m, q, :].rearrange("r (p j) -> r p j", j=PACK)
+                    shuffled = delta_ps[:].rearrange("r (j p) -> r p j", j=PACK)
+                    if q == N_BANKS - 1:
+                        nc.vector.tensor_scalar_mul(out=ordered, in0=shuffled, scalar1=LORA_SCALE)
+                    else:
+                        nc.scalar.mul(out=ordered, in_=shuffled, mul=LORA_SCALE)
+
+        h_bf16 = {}
+
+        def gate_up(e, m):
+            rounded = work.tile([P, D_PASSES, PACK, P], BF16, tag="h_bf16")
+            h_bf16[(e, m)] = rounded
+            h_rows = out_0[e].rearrange("(p m) d -> p m d", m=TOKEN_TILES)
+            for c in range(D_PASSES):
+                base = []
+                for q in (c, D_PASSES + c):
+                    acc = psum.tile([P, BANK], F32, tag="base", bufs=4)
+                    for kc in range(H_PASSES):
+                        g = H_PASSES * e + kc
+                        offset = 4 * (g % PLANES_PER_TILE)
+                        nc.tensor.matmul_mx(
+                            out=acc[:],
+                            lhsT=x_words[e][:, kc, m, :].bitcast(FP8X4),
+                            lhsT_scale=x_planes[e][:, kc, m, :],
+                            rhs=w_words[g][:, BANK * q : BANK * (q + 1)].bitcast(FP8X4),
+                            rhs_scale=w_planes[g // PLANES_PER_TILE][offset:P, BANK * q : BANK * (q + 1)],
+                            start=(kc == 0),
+                            stop=(kc == H_PASSES - 1),
+                        )
+                    base.append(acc)
+                gate = work.tile([P, BANK], F32, tag="gate", bufs=3)
+                nc.vector.tensor_tensor(out=gate[:], in0=base[0][:], in1=delta2[e][:, m, c, :], op=ALU.add)
+                nc.scalar.activation(out=gate[:], in_=gate[:], func=ACT.Silu)
+                up = work.tile([P, BANK], F32, tag="up", bufs=3)
+                nc.vector.tensor_tensor(out=up[:], in0=base[1][:], in1=delta2[e][:, m, D_PASSES + c, :], op=ALU.add)
+                h = work.tile([P, BANK], F32, tag="h", bufs=3)
+                nc.gpsimd.tensor_tensor(out=h[:], in0=up[:], in1=gate[:], op=ALU.mult)
+                nc.sync.dma_start(out=h_rows[:, m, BANK * c : BANK * (c + 1)], in_=h[:])
+                nc.gpsimd.tensor_scalar(
+                    out=h_bf16[(e, m)][:, c],
+                    in0=h[:].rearrange("r (p t) -> r t p", t=PACK),
+                    scalar1=1.0,
+                    scalar2=0.0,
+                    op0=ALU.mult,
+                    op1=ALU.add,
+                )
+
+        low_d_sb = {}
+
+        def low_rank(e, m):
+            h_ps = psum.tile([P, D_PASSES, PACK, P], BF16, tag="tr")
+            for c in range(D_PASSES):
+                for t in range(PACK):
+                    nc.tensor.transpose(h_ps[:, c, t, :], h_bf16[(e, m)][:, c, t, :], ident_bf16[:])
+            h_grouped = work.tile([P, D_PASSES, P, PACK], BF16, tag="h_grouped", align_bytes=64)
+            nc.scalar.copy(out=h_grouped[:], in_=h_ps[:].rearrange("p c t r -> p c r t"))
+            h_words = work.tile([P, D_PASSES, P], U32, tag="h_words", align_bytes=64)
+            h_planes = work.tile([P, D_PASSES, P], U8, tag="h_planes", align_bytes=64)
+            nc.vector.quantize_mx(
+                out=h_words[:].rearrange("p c r -> p (c r)").bitcast(FP8X4),
+                scales=h_planes[:].rearrange("p c r -> p (c r)"),
+                in_=h_grouped[:].rearrange("p c r t -> p (c r t)"),
+            )
+            low_d_ps = psum.tile([P, R], F32, tag="tr")
+            for c in range(D_PASSES):
+                nc.tensor.matmul_mx(
+                    out=low_d_ps[:],
+                    lhsT=h_words[:, c, :].bitcast(FP8X4),
+                    lhsT_scale=h_planes[:, c, :],
+                    rhs=a_words[:, D_PASSES * e + c, :].bitcast(FP8X4),
+                    rhs_scale=a_planes[:, D_PASSES * e + c, :],
+                    start=(c == 0),
+                    stop=(c == D_PASSES - 1),
+                )
+            if m == 0:
+                both_tiles = work.tile([P, TOKEN_TILES, R], F32, tag="low_d_sb")
+                low_d_sb[e] = both_tiles
+            nc.vector.tensor_copy(out=low_d_sb[e][:, m, :], in_=low_d_ps[:])
+            if m == TOKEN_TILES - 1:
+                nc.sync.dma_start(out=out_1[e].rearrange("(p m) r -> p m r", m=TOKEN_TILES), in_=low_d_sb[e][:])
+
+        prepare(0)
+        prepare(1)
+        previous = None
+        for e in range(E):
+            for m in range(TOKEN_TILES):
+                gate_up(e, m)
+                if previous is not None:
+                    low_rank(previous[0], previous[1])
+                previous = (e, m)
+            if e + 2 < E:
+                prepare(e + 2)
+        low_rank(previous[0], previous[1])

@@ -23,6 +23,7 @@ D_PASSES = D // K_PASS
 N_BANKS = 2 * D // BANK
 PLANES_PER_TILE = 4
 LORA_SCALE = 2.0
+ROWS = E * TOKEN_TILES
 
 FLOPS = 2 * E * T * (2 * D) * H + 2 * E * T * (2 * D) * R + 2 * E * T * D * R
 
@@ -34,13 +35,15 @@ def tile_loralinearexpertswrapper_pa_e_kernel(
     with ExitStack() as ctx:
         keep = ctx.enter_context(tc.tile_pool(name="keep", bufs=1))
         work = ctx.enter_context(tc.tile_pool(name="work", bufs=2))
-        psum = ctx.enter_context(tc.psum_pool(name="psum", bufs=2))
+        psum = ctx.enter_context(tc.psum_pool(name="psum", bufs=1))
+        ctx.enter_context(tc.manual_schedule())
 
         x_sb = [keep.tile([P, TOKEN_TILES, H], BF16, name="x_sb%d" % e) for e in range(E)]
         low_sb = keep.tile([P, E, TOKEN_TILES, R], BF16, name="low_sb")
         b_sb = [keep.tile([P, N_BANKS, PACK, R], BF16, name="b_sb%d" % e) for e in range(E)]
         w_words = [
-            keep.tile([P, 2 * D], U32, name="w_words%d" % g, align_bytes=64) for g in range(E * H_PASSES)
+            [keep.tile([P, 2, BANK], U32, name="w_words%d_%d" % (g, c), align_bytes=64) for c in range(D_PASSES)]
+            for g in range(E * H_PASSES)
         ]
         w_planes = [
             keep.tile([P, 2 * D], U8, name="w_planes%d" % b, align_bytes=64)
@@ -53,16 +56,21 @@ def tile_loralinearexpertswrapper_pa_e_kernel(
             nc.vector.memset(plane_tile[:].bitcast(I32), 0)
         nc.vector.memset(a_planes[:].rearrange("p g n -> p (g n)").bitcast(I32), 0)
 
-        ident_bf16 = keep.tile([P, P], BF16, name="ident_bf16")
-        make_identity(nc, ident_bf16[:])
+        warm = keep.tile([P, 2], F32, name="warm")
+        nc.vector.memset(warm[:, 0:1], 0.0)
+        nc.scalar.activation(out=warm[:, 1:2], in_=warm[:, 0:1], func=ACT.Silu)
+
         ident_f32 = keep.tile([P, P], F32, name="ident_f32")
         make_identity(nc, ident_f32[:])
+        ident_bf16 = keep.tile([P, P], BF16, name="ident_bf16")
+        make_identity(nc, ident_bf16[:])
 
-        def load_tokens(e):
+        def load_x(e):
             nc.sync.dma_start(out=x_sb[e][:], in_=x[e].rearrange("(p m) k -> p m k", m=TOKEN_TILES))
+
+        def load_b(e):
             nc.sync.dma_start(
-                out=b_sb[e][:],
-                in_=B_gu[e].rearrange("(q p j) r -> p q j r", q=N_BANKS, p=P, j=PACK),
+                out=b_sb[e][:], in_=B_gu[e].rearrange("(q p j) r -> p q j r", q=N_BANKS, p=P, j=PACK)
             )
 
         def load_w_planes(b):
@@ -74,162 +82,191 @@ def tile_loralinearexpertswrapper_pa_e_kernel(
                     ].bitcast(I32),
                 )
 
-        def load_a_planes():
+        def load_a():
+            nc.sync.dma_start(
+                out=a_words[:].bitcast(I32), in_=A_d_words.rearrange("g p n t -> p g (n t)").bitcast(I32)
+            )
             for quadrant in range(4):
                 nc.sync.dma_start(
                     out=a_planes[32 * quadrant : 32 * quadrant + 4, :, :].bitcast(I32),
                     in_=A_d_scales[:, 4 * quadrant : 4 * quadrant + 4, :].rearrange("g r n -> r g n").bitcast(I32),
                 )
 
-        def load_w_words(e):
+        def load_w_words(e, c):
             for kc in range(H_PASSES):
                 g = H_PASSES * e + kc
-                nc.sync.dma_start(
-                    out=w_words[g][:].bitcast(I32),
-                    in_=W_gu_words[g].rearrange("p n t -> p (n t)").bitcast(I32),
+                pieces = (
+                    W_gu_words[g]
+                    .rearrange("p n t -> p (n t)")
+                    .bitcast(I32)
+                    .rearrange("p (half c n) -> p half c n", half=2, c=D_PASSES)
                 )
+                nc.sync.dma_start(out=w_words[g][c][:].bitcast(I32), in_=pieces[:, :, c, :])
 
-        load_tokens(0)
+        load_x(0)
+        load_b(0)
         nc.sync.dma_start(out=low_sb[:], in_=low_gu.rearrange("e (p m) r -> p e m r", m=TOKEN_TILES))
         load_w_planes(0)
-        load_w_planes(1)
-        load_a_planes()
-        load_tokens(1)
-        load_w_words(0)
-        nc.sync.dma_start(
-            out=a_words[:].bitcast(I32), in_=A_d_words.rearrange("g p n t -> p g (n t)").bitcast(I32)
-        )
-        load_tokens(2)
-        load_w_words(1)
-        load_tokens(3)
-        load_w_words(2)
-        load_w_words(3)
-
-        low_t = keep.tile([P, E, TOKEN_TILES, P], BF16, name="low_t")
-        low_ps = psum.tile([P, E, TOKEN_TILES, P], BF16, tag="tr")
         for e in range(E):
-            for m in range(TOKEN_TILES):
-                nc.tensor.transpose(low_ps[:, e, m, :], low_sb[:, e, m, :], ident_bf16[:])
-        nc.vector.tensor_copy(out=low_t[:], in_=low_ps[:])
+            load_w_words(e, 0)
+            if e + 1 < E:
+                load_b(e + 1)
+            load_w_words(e, 1)
+            if e + 1 < E:
+                load_x(e + 1)
+            if e == 0:
+                load_a()
+                load_w_planes(1)
 
+        x_grouped = {}
         x_words = {}
         x_planes = {}
+        b_t = {}
         delta2 = {}
+        h_bf16 = {}
+        h_grouped = {}
+        h_words = {}
+        h_planes = {}
+        low_d_sb = {}
 
-        def prepare(e):
+        def transpose_x(e):
             x_pairs = x_sb[e][:].rearrange("p m k -> p (m k)").bitcast(F32)
-            x_grouped = work.tile([P, H_PASSES, TOKEN_TILES, P, PACK], BF16, tag="x_grouped", align_bytes=64)
+            grouped = work.tile([P, H_PASSES, TOKEN_TILES, P, PACK], BF16, tag="x_grouped", align_bytes=64)
+            x_grouped[e] = grouped
             for kc in range(H_PASSES):
-                x_ps = psum.tile([P, TOKEN_TILES, 2, P], F32, tag="tr")
+                x_ps = psum.tile([P, TOKEN_TILES, 2, P], F32, tag="aux", bufs=5)
                 for m in range(TOKEN_TILES):
                     for u in range(2):
                         first = (H // 2) * m + (K_PASS // 2) * kc
                         nc.tensor.transpose(
                             x_ps[:, m, u, :], x_pairs[:, first + u : first + K_PASS // 2 : 2], ident_f32[:]
                         )
-                nc.vector.tensor_copy(
-                    out=x_grouped[:, kc]
+                nc.scalar.copy(
+                    out=grouped[:, kc]
                     .rearrange("p m r t -> p (m r t)")
                     .bitcast(F32)
                     .rearrange("p (m r u) -> p m r u", m=TOKEN_TILES, u=2),
                     in_=x_ps[:].rearrange("p m u r -> p m r u"),
                 )
-            words = work.tile([P, H_PASSES, TOKEN_TILES, P], U32, tag="x_words", bufs=3, align_bytes=64)
-            planes = work.tile([P, H_PASSES, TOKEN_TILES, P], U8, tag="x_planes", bufs=3, align_bytes=64)
+
+        def quantise_x(e):
+            words = work.tile([P, H_PASSES, TOKEN_TILES, P], U32, tag="x_words", align_bytes=64)
+            planes = work.tile([P, H_PASSES, TOKEN_TILES, P], U8, tag="x_planes", align_bytes=64)
             x_words[e] = words
             x_planes[e] = planes
+            nc.vector.quantize_mx(
+                out=words[:].rearrange("p c m r -> p (c m r)").bitcast(FP8X4),
+                scales=planes[:].rearrange("p c m r -> p (c m r)"),
+                in_=x_grouped[e][:].rearrange("p c m r t -> p (c m r t)"),
+            )
 
-            b_t = work.tile([P, N_BANKS, PACK * P], BF16, tag="b_t")
+        def transpose_b(e):
+            flipped = work.tile([P, N_BANKS, PACK * P], BF16, tag="b_t")
+            b_t[e] = flipped
             for half in range(2):
-                b_ps = psum.tile([P, 2, PACK, P], BF16, tag="tr")
+                b_ps = psum.tile([P, 2, PACK, P], BF16, tag="aux", bufs=5)
                 for i in range(2):
                     for j in range(PACK):
                         nc.tensor.transpose(b_ps[:, i, j, :], b_sb[e][:, 2 * half + i, j, :], ident_bf16[:])
                 nc.scalar.copy(
-                    out=b_t[:, 2 * half : 2 * half + 2, :], in_=b_ps[:].rearrange("r i j p -> r i (j p)")
+                    out=flipped[:, 2 * half : 2 * half + 2, :], in_=b_ps[:].rearrange("r i j p -> r i (j p)")
                 )
 
-            nc.vector.quantize_mx(
-                out=x_words[e][:].rearrange("p c m r -> p (c m r)").bitcast(FP8X4),
-                scales=x_planes[e][:].rearrange("p c m r -> p (c m r)"),
-                in_=x_grouped[:].rearrange("p c m r t -> p (c m r t)"),
+        low_t = keep.tile([P, E, TOKEN_TILES, P], BF16, name="low_t")
+
+        def transpose_low():
+            low_ps = psum.tile([P, E, TOKEN_TILES, P], BF16, tag="aux", bufs=5)
+            for e in range(E):
+                for m in range(TOKEN_TILES):
+                    nc.tensor.transpose(low_ps[:, e, m, :], low_sb[:, e, m, :], ident_bf16[:])
+            nc.vector.tensor_copy(out=low_t[:], in_=low_ps[:])
+
+        def lora_delta(e, m, c):
+            if m == 0 and c == 0:
+                doubled = work.tile([P, TOKEN_TILES, N_BANKS, BANK], F32, tag="delta2")
+                delta2[e] = doubled
+            banks = []
+            for q in (c, D_PASSES + c):
+                delta_ps = psum.tile([P, BANK], F32, tag="aux", bufs=5)
+                nc.tensor.matmul(delta_ps[:], lhsT=low_t[:, e, m, :], rhs=b_t[e][:, q, :], start=True, stop=True)
+                banks.append(delta_ps)
+            nc.scalar.mul(
+                out=delta2[e][:, m, c, :].rearrange("r (p j) -> r p j", j=PACK),
+                in_=banks[0][:].rearrange("r (j p) -> r p j", j=PACK),
+                mul=LORA_SCALE,
+            )
+            nc.vector.tensor_scalar_mul(
+                out=delta2[e][:, m, D_PASSES + c, :].rearrange("r (p j) -> r p j", j=PACK),
+                in0=banks[1][:].rearrange("r (j p) -> r p j", j=PACK),
+                scalar1=LORA_SCALE,
             )
 
-            doubled = work.tile([P, TOKEN_TILES, N_BANKS, BANK], F32, tag="delta2", bufs=3)
-            delta2[e] = doubled
-            for m in range(TOKEN_TILES):
-                for q in range(N_BANKS):
-                    delta_ps = psum.tile([P, BANK], F32, tag="delta")
-                    nc.tensor.matmul(delta_ps[:], lhsT=low_t[:, e, m, :], rhs=b_t[:, q, :], start=True, stop=True)
-                    ordered = delta2[e][:, m, q, :].rearrange("r (p j) -> r p j", j=PACK)
-                    shuffled = delta_ps[:].rearrange("r (j p) -> r p j", j=PACK)
-                    if q == N_BANKS - 1:
-                        nc.vector.tensor_scalar_mul(out=ordered, in0=shuffled, scalar1=LORA_SCALE)
-                    else:
-                        nc.scalar.mul(out=ordered, in_=shuffled, mul=LORA_SCALE)
-
-        h_bf16 = {}
-
-        def gate_up(e, m):
-            rounded = work.tile([P, D_PASSES, PACK, P], BF16, tag="h_bf16")
-            h_bf16[(e, m)] = rounded
+        def gate_up(e, m, c):
+            base = []
+            for half in range(2):
+                acc = psum.tile([P, BANK], F32, tag="base", bufs=3)
+                for kc in range(H_PASSES):
+                    g = H_PASSES * e + kc
+                    offset = 4 * (g % PLANES_PER_TILE)
+                    first = D * half + BANK * c
+                    nc.tensor.matmul_mx(
+                        out=acc[:],
+                        lhsT=x_words[e][:, kc, m, :].bitcast(FP8X4),
+                        lhsT_scale=x_planes[e][:, kc, m, :],
+                        rhs=w_words[g][c][:, half, :].bitcast(FP8X4),
+                        rhs_scale=w_planes[g // PLANES_PER_TILE][offset:P, first : first + BANK],
+                        start=(kc == 0),
+                        stop=(kc == H_PASSES - 1),
+                    )
+                base.append(acc)
+            gate = work.tile([P, BANK], F32, tag="gate", bufs=3)
+            nc.vector.tensor_tensor(out=gate[:], in0=base[0][:], in1=delta2[e][:, m, c, :], op=ALU.add)
+            nc.scalar.activation(out=gate[:], in_=gate[:], func=ACT.Silu)
+            up = work.tile([P, BANK], F32, tag="up", bufs=3)
+            nc.vector.tensor_tensor(out=up[:], in0=base[1][:], in1=delta2[e][:, m, D_PASSES + c, :], op=ALU.add)
+            h = work.tile([P, BANK], F32, tag="h", bufs=10)
+            nc.gpsimd.tensor_tensor(out=h[:], in0=up[:], in1=gate[:], op=ALU.mult)
             h_rows = out_0[e].rearrange("(p m) d -> p m d", m=TOKEN_TILES)
-            for c in range(D_PASSES):
-                base = []
-                for q in (c, D_PASSES + c):
-                    acc = psum.tile([P, BANK], F32, tag="base", bufs=4)
-                    for kc in range(H_PASSES):
-                        g = H_PASSES * e + kc
-                        offset = 4 * (g % PLANES_PER_TILE)
-                        nc.tensor.matmul_mx(
-                            out=acc[:],
-                            lhsT=x_words[e][:, kc, m, :].bitcast(FP8X4),
-                            lhsT_scale=x_planes[e][:, kc, m, :],
-                            rhs=w_words[g][:, BANK * q : BANK * (q + 1)].bitcast(FP8X4),
-                            rhs_scale=w_planes[g // PLANES_PER_TILE][offset:P, BANK * q : BANK * (q + 1)],
-                            start=(kc == 0),
-                            stop=(kc == H_PASSES - 1),
-                        )
-                    base.append(acc)
-                gate = work.tile([P, BANK], F32, tag="gate", bufs=3)
-                nc.vector.tensor_tensor(out=gate[:], in0=base[0][:], in1=delta2[e][:, m, c, :], op=ALU.add)
-                nc.scalar.activation(out=gate[:], in_=gate[:], func=ACT.Silu)
-                up = work.tile([P, BANK], F32, tag="up", bufs=3)
-                nc.vector.tensor_tensor(out=up[:], in0=base[1][:], in1=delta2[e][:, m, D_PASSES + c, :], op=ALU.add)
-                h = work.tile([P, BANK], F32, tag="h", bufs=3)
-                nc.gpsimd.tensor_tensor(out=h[:], in0=up[:], in1=gate[:], op=ALU.mult)
-                nc.sync.dma_start(out=h_rows[:, m, BANK * c : BANK * (c + 1)], in_=h[:])
-                nc.gpsimd.tensor_scalar(
-                    out=h_bf16[(e, m)][:, c],
-                    in0=h[:].rearrange("r (p t) -> r t p", t=PACK),
-                    scalar1=1.0,
-                    scalar2=0.0,
-                    op0=ALU.mult,
-                    op1=ALU.add,
-                )
+            nc.sync.dma_start(out=h_rows[:, m, BANK * c : BANK * (c + 1)], in_=h[:])
+            if c == 0:
+                rounded = work.tile([P, D_PASSES, PACK, P], BF16, tag="h_bf16", bufs=3)
+                h_bf16[(e, m)] = rounded
+            nc.gpsimd.tensor_scalar(
+                out=h_bf16[(e, m)][:, c],
+                in0=h[:].rearrange("r (p t) -> r t p", t=PACK),
+                scalar1=1.0,
+                scalar2=0.0,
+                op0=ALU.mult,
+                op1=ALU.add,
+            )
 
-        low_d_sb = {}
-
-        def low_rank(e, m):
-            h_ps = psum.tile([P, D_PASSES, PACK, P], BF16, tag="tr")
+        def transpose_h(e, m):
+            h_ps = psum.tile([P, D_PASSES, PACK, P], BF16, tag="aux", bufs=5)
             for c in range(D_PASSES):
                 for t in range(PACK):
                     nc.tensor.transpose(h_ps[:, c, t, :], h_bf16[(e, m)][:, c, t, :], ident_bf16[:])
-            h_grouped = work.tile([P, D_PASSES, P, PACK], BF16, tag="h_grouped", align_bytes=64)
-            nc.scalar.copy(out=h_grouped[:], in_=h_ps[:].rearrange("p c t r -> p c r t"))
-            h_words = work.tile([P, D_PASSES, P], U32, tag="h_words", align_bytes=64)
-            h_planes = work.tile([P, D_PASSES, P], U8, tag="h_planes", align_bytes=64)
+            grouped = work.tile([P, D_PASSES, P, PACK], BF16, tag="h_grouped", align_bytes=64)
+            h_grouped[(e, m)] = grouped
+            nc.scalar.copy(out=grouped[:], in_=h_ps[:].rearrange("p c t r -> p c r t"))
+
+        def quantise_h(e, m):
+            words = work.tile([P, D_PASSES, P], U32, tag="h_words", align_bytes=64)
+            planes = work.tile([P, D_PASSES, P], U8, tag="h_planes", align_bytes=64)
+            h_words[(e, m)] = words
+            h_planes[(e, m)] = planes
             nc.vector.quantize_mx(
-                out=h_words[:].rearrange("p c r -> p (c r)").bitcast(FP8X4),
-                scales=h_planes[:].rearrange("p c r -> p (c r)"),
-                in_=h_grouped[:].rearrange("p c r t -> p (c r t)"),
+                out=words[:].rearrange("p c r -> p (c r)").bitcast(FP8X4),
+                scales=planes[:].rearrange("p c r -> p (c r)"),
+                in_=h_grouped[(e, m)][:].rearrange("p c r t -> p (c r t)"),
             )
-            low_d_ps = psum.tile([P, R], F32, tag="tr")
+
+        def low_rank(e, m):
+            low_d_ps = psum.tile([P, R], F32, tag="aux", bufs=5)
             for c in range(D_PASSES):
                 nc.tensor.matmul_mx(
                     out=low_d_ps[:],
-                    lhsT=h_words[:, c, :].bitcast(FP8X4),
-                    lhsT_scale=h_planes[:, c, :],
+                    lhsT=h_words[(e, m)][:, c, :].bitcast(FP8X4),
+                    lhsT_scale=h_planes[(e, m)][:, c, :],
                     rhs=a_words[:, D_PASSES * e + c, :].bitcast(FP8X4),
                     rhs_scale=a_planes[:, D_PASSES * e + c, :],
                     start=(c == 0),
@@ -242,15 +279,32 @@ def tile_loralinearexpertswrapper_pa_e_kernel(
             if m == TOKEN_TILES - 1:
                 nc.sync.dma_start(out=out_1[e].rearrange("(p m) r -> p m r", m=TOKEN_TILES), in_=low_d_sb[e][:])
 
-        prepare(0)
-        prepare(1)
-        previous = None
-        for e in range(E):
-            for m in range(TOKEN_TILES):
-                gate_up(e, m)
-                if previous is not None:
-                    low_rank(previous[0], previous[1])
-                previous = (e, m)
-            if e + 2 < E:
-                prepare(e + 2)
-        low_rank(previous[0], previous[1])
+        transpose_x(0)
+        quantise_x(0)
+        transpose_b(0)
+        transpose_low()
+        for m in range(TOKEN_TILES):
+            for c in range(D_PASSES):
+                lora_delta(0, m, c)
+        transpose_b(1)
+
+        for row in range(ROWS + 2):
+            e, m = divmod(row, TOKEN_TILES)
+            for c in range(D_PASSES):
+                if row < ROWS:
+                    gate_up(e, m, c)
+                    if e + 1 < E:
+                        lora_delta(e + 1, m, c)
+                if c == 0:
+                    if row >= 2:
+                        quantise_h((row - 2) // TOKEN_TILES, (row - 2) % TOKEN_TILES)
+                    if m == 1 and e + 1 < E:
+                        quantise_x(e + 1)
+            if row >= 2:
+                low_rank((row - 2) // TOKEN_TILES, (row - 2) % TOKEN_TILES)
+            if m == 0 and e + 1 < E:
+                transpose_x(e + 1)
+            if m == 1 and e + 2 < E:
+                transpose_b(e + 2)
+            if 1 <= row <= ROWS:
+                transpose_h((row - 1) // TOKEN_TILES, (row - 1) % TOKEN_TILES)

@@ -42,7 +42,7 @@ def tile_loralinearexpertswrapper_pa_e_kernel(
         low_sb = keep.tile([P, E, TOKEN_TILES, R], BF16, name="low_sb")
         b_sb = [keep.tile([P, N_BANKS, PACK, R], BF16, name="b_sb%d" % e) for e in range(E)]
         w_words = [
-            [keep.tile([P, 2, BANK], U32, name="w_words%d_%d" % (g, c), align_bytes=64) for c in range(D_PASSES)]
+            keep.tile([P, 2, D_PASSES, BANK], U32, name="w_words%d" % g, align_bytes=64)
             for g in range(E * H_PASSES)
         ]
         w_planes = [
@@ -92,7 +92,7 @@ def tile_loralinearexpertswrapper_pa_e_kernel(
                     in_=A_d_scales[:, 4 * quadrant : 4 * quadrant + 4, :].rearrange("g r n -> r g n").bitcast(I32),
                 )
 
-        def load_w_words(e, c):
+        def load_w_piece(e, c):
             for kc in range(H_PASSES):
                 g = H_PASSES * e + kc
                 pieces = (
@@ -101,28 +101,41 @@ def tile_loralinearexpertswrapper_pa_e_kernel(
                     .bitcast(I32)
                     .rearrange("p (half c n) -> p half c n", half=2, c=D_PASSES)
                 )
-                nc.sync.dma_start(out=w_words[g][c][:].bitcast(I32), in_=pieces[:, :, c, :])
+                nc.sync.dma_start(out=w_words[g][:, :, c, :].bitcast(I32), in_=pieces[:, :, c, :])
+
+        def load_w_words(e):
+            for kc in range(H_PASSES):
+                g = H_PASSES * e + kc
+                nc.sync.dma_start(
+                    out=w_words[g][:].rearrange("p half c n -> p (half c n)").bitcast(I32),
+                    in_=W_gu_words[g].rearrange("p n t -> p (n t)").bitcast(I32),
+                )
 
         load_x(0)
         load_b(0)
         nc.sync.dma_start(out=low_sb[:], in_=low_gu.rearrange("e (p m) r -> p e m r", m=TOKEN_TILES))
         load_w_planes(0)
-        for e in range(E):
-            load_w_words(e, 0)
-            if e + 1 < E:
-                load_b(e + 1)
-            load_w_words(e, 1)
-            if e + 1 < E:
-                load_x(e + 1)
-            if e == 0:
-                load_a()
-                load_w_planes(1)
+        load_w_piece(0, 0)
+        load_b(1)
+        load_w_piece(0, 1)
+        load_x(1)
+        load_b(2)
+        load_w_words(1)
+        load_a()
+        load_x(2)
+        load_b(3)
+        load_w_planes(1)
+        load_w_words(2)
+        load_x(3)
+        load_w_words(3)
 
         x_grouped = {}
         x_words = {}
         x_planes = {}
         b_t = {}
         delta2 = {}
+        delta_banks = {}
+        base_banks = {}
         h_bf16 = {}
         h_grouped = {}
         h_words = {}
@@ -181,28 +194,30 @@ def tile_loralinearexpertswrapper_pa_e_kernel(
                     nc.tensor.transpose(low_ps[:, e, m, :], low_sb[:, e, m, :], ident_bf16[:])
             nc.vector.tensor_copy(out=low_t[:], in_=low_ps[:])
 
-        def lora_delta(e, m, c):
+        def lora_products(e, m, c):
             if m == 0 and c == 0:
                 doubled = work.tile([P, TOKEN_TILES, N_BANKS, BANK], F32, tag="delta2")
                 delta2[e] = doubled
-            banks = []
             for q in (c, D_PASSES + c):
                 delta_ps = psum.tile([P, BANK], F32, tag="aux", bufs=5)
                 nc.tensor.matmul(delta_ps[:], lhsT=low_t[:, e, m, :], rhs=b_t[e][:, q, :], start=True, stop=True)
-                banks.append(delta_ps)
+                delta_banks[(e, m, q)] = delta_ps
+
+        def lora_gate_out(e, m, c):
             nc.scalar.mul(
                 out=delta2[e][:, m, c, :].rearrange("r (p j) -> r p j", j=PACK),
-                in_=banks[0][:].rearrange("r (j p) -> r p j", j=PACK),
+                in_=delta_banks[(e, m, c)][:].rearrange("r (j p) -> r p j", j=PACK),
                 mul=LORA_SCALE,
             )
+
+        def lora_up_out(e, m, c):
             nc.vector.tensor_scalar_mul(
                 out=delta2[e][:, m, D_PASSES + c, :].rearrange("r (p j) -> r p j", j=PACK),
-                in0=banks[1][:].rearrange("r (j p) -> r p j", j=PACK),
+                in0=delta_banks[(e, m, D_PASSES + c)][:].rearrange("r (j p) -> r p j", j=PACK),
                 scalar1=LORA_SCALE,
             )
 
-        def gate_up(e, m, c):
-            base = []
+        def gate_up_passes(e, m, c):
             for half in range(2):
                 acc = psum.tile([P, BANK], F32, tag="base", bufs=3)
                 for kc in range(H_PASSES):
@@ -213,41 +228,61 @@ def tile_loralinearexpertswrapper_pa_e_kernel(
                         out=acc[:],
                         lhsT=x_words[e][:, kc, m, :].bitcast(FP8X4),
                         lhsT_scale=x_planes[e][:, kc, m, :],
-                        rhs=w_words[g][c][:, half, :].bitcast(FP8X4),
+                        rhs=w_words[g][:, half, c, :].bitcast(FP8X4),
                         rhs_scale=w_planes[g // PLANES_PER_TILE][offset:P, first : first + BANK],
                         start=(kc == 0),
                         stop=(kc == H_PASSES - 1),
                     )
-                base.append(acc)
+                base_banks[(e, m, c, half)] = acc
+
+        def swiglu(e, m, c, with_lora):
             gate = work.tile([P, BANK], F32, tag="gate", bufs=3)
-            nc.vector.tensor_tensor(out=gate[:], in0=base[0][:], in1=delta2[e][:, m, c, :], op=ALU.add)
+            nc.vector.tensor_tensor(
+                out=gate[:], in0=base_banks[(e, m, c, 0)][:], in1=delta2[e][:, m, c, :], op=ALU.add
+            )
+            if with_lora:
+                lora_gate_out(e + 1, m, c)
             nc.scalar.activation(out=gate[:], in_=gate[:], func=ACT.Silu)
             up = work.tile([P, BANK], F32, tag="up", bufs=3)
-            nc.vector.tensor_tensor(out=up[:], in0=base[1][:], in1=delta2[e][:, m, D_PASSES + c, :], op=ALU.add)
+            nc.vector.tensor_tensor(
+                out=up[:], in0=base_banks[(e, m, c, 1)][:], in1=delta2[e][:, m, D_PASSES + c, :], op=ALU.add
+            )
             h = work.tile([P, BANK], F32, tag="h", bufs=10)
             nc.gpsimd.tensor_tensor(out=h[:], in0=up[:], in1=gate[:], op=ALU.mult)
             h_rows = out_0[e].rearrange("(p m) d -> p m d", m=TOKEN_TILES)
             nc.sync.dma_start(out=h_rows[:, m, BANK * c : BANK * (c + 1)], in_=h[:])
             if c == 0:
-                rounded = work.tile([P, D_PASSES, PACK, P], BF16, tag="h_bf16", bufs=3)
+                rounded = work.tile([P, D_PASSES, 2, P, 2], BF16, tag="h_bf16", bufs=3)
                 h_bf16[(e, m)] = rounded
             nc.gpsimd.tensor_scalar(
                 out=h_bf16[(e, m)][:, c],
-                in0=h[:].rearrange("r (p t) -> r t p", t=PACK),
+                in0=h[:].rearrange("r (p u i) -> r u p i", u=2, i=2),
                 scalar1=1.0,
                 scalar2=0.0,
                 op0=ALU.mult,
                 op1=ALU.add,
             )
+            if with_lora:
+                lora_up_out(e + 1, m, c)
 
         def transpose_h(e, m):
-            h_ps = psum.tile([P, D_PASSES, PACK, P], BF16, tag="aux", bufs=5)
+            h_ps = psum.tile([P, D_PASSES, 2, P], F32, tag="aux", bufs=5)
             for c in range(D_PASSES):
-                for t in range(PACK):
-                    nc.tensor.transpose(h_ps[:, c, t, :], h_bf16[(e, m)][:, c, t, :], ident_bf16[:])
+                for u in range(2):
+                    nc.tensor.transpose(
+                        h_ps[:, c, u, :],
+                        h_bf16[(e, m)][:, c, u].rearrange("r p i -> r (p i)").bitcast(F32),
+                        ident_f32[:],
+                    )
             grouped = work.tile([P, D_PASSES, P, PACK], BF16, tag="h_grouped", align_bytes=64)
             h_grouped[(e, m)] = grouped
-            nc.scalar.copy(out=grouped[:], in_=h_ps[:].rearrange("p c t r -> p c r t"))
+            nc.scalar.copy(
+                out=grouped[:]
+                .rearrange("p c r t -> p (c r t)")
+                .bitcast(F32)
+                .rearrange("p (c r u) -> p c r u", c=D_PASSES, u=2),
+                in_=h_ps[:].rearrange("p c u r -> p c r u"),
+            )
 
         def quantise_h(e, m):
             words = work.tile([P, D_PASSES, P], U32, tag="h_words", align_bytes=64)
@@ -285,16 +320,19 @@ def tile_loralinearexpertswrapper_pa_e_kernel(
         transpose_low()
         for m in range(TOKEN_TILES):
             for c in range(D_PASSES):
-                lora_delta(0, m, c)
+                lora_products(0, m, c)
+                lora_gate_out(0, m, c)
+                lora_up_out(0, m, c)
         transpose_b(1)
 
         for row in range(ROWS + 2):
             e, m = divmod(row, TOKEN_TILES)
             for c in range(D_PASSES):
                 if row < ROWS:
-                    gate_up(e, m, c)
+                    gate_up_passes(e, m, c)
                     if e + 1 < E:
-                        lora_delta(e + 1, m, c)
+                        lora_products(e + 1, m, c)
+                    swiglu(e, m, c, e + 1 < E)
                 if c == 0:
                     if row >= 2:
                         quantise_h((row - 2) // TOKEN_TILES, (row - 2) % TOKEN_TILES)

@@ -203,17 +203,17 @@ def tile_loralinearexpertswrapper_pa_e_kernel(
                 nc.tensor.matmul(delta_ps[:], lhsT=low_t[:, e, m, :], rhs=b_t[e][:, q, :], start=True, stop=True)
                 delta_banks[(e, m, q)] = delta_ps
 
-        def lora_gate_out(e, m, c):
+        def lora_out_scalar(e, m, q):
             nc.scalar.mul(
-                out=delta2[e][:, m, c, :].rearrange("r (p j) -> r p j", j=PACK),
-                in_=delta_banks[(e, m, c)][:].rearrange("r (j p) -> r p j", j=PACK),
+                out=delta2[e][:, m, q, :].rearrange("r (p j) -> r p j", j=PACK),
+                in_=delta_banks[(e, m, q)][:].rearrange("r (j p) -> r p j", j=PACK),
                 mul=LORA_SCALE,
             )
 
-        def lora_up_out(e, m, c):
+        def lora_out_vector(e, m, q):
             nc.vector.tensor_scalar_mul(
-                out=delta2[e][:, m, D_PASSES + c, :].rearrange("r (p j) -> r p j", j=PACK),
-                in0=delta_banks[(e, m, D_PASSES + c)][:].rearrange("r (j p) -> r p j", j=PACK),
+                out=delta2[e][:, m, q, :].rearrange("r (p j) -> r p j", j=PACK),
+                in0=delta_banks[(e, m, q)][:].rearrange("r (j p) -> r p j", j=PACK),
                 scalar1=LORA_SCALE,
             )
 
@@ -241,14 +241,19 @@ def tile_loralinearexpertswrapper_pa_e_kernel(
                 out=gate[:], in0=base_banks[(e, m, c, 0)][:], in1=delta2[e][:, m, c, :], op=ALU.add
             )
             if with_lora:
-                lora_gate_out(e + 1, m, c)
+                lora_out_scalar(e + 1, m, c)
             nc.scalar.activation(out=gate[:], in_=gate[:], func=ACT.Silu)
             up = work.tile([P, BANK], F32, tag="up", bufs=3)
             nc.vector.tensor_tensor(
                 out=up[:], in0=base_banks[(e, m, c, 1)][:], in1=delta2[e][:, m, D_PASSES + c, :], op=ALU.add
             )
             h = work.tile([P, BANK], F32, tag="h", bufs=10)
-            nc.gpsimd.tensor_tensor(out=h[:], in0=up[:], in1=gate[:], op=ALU.mult)
+            if c == 0:
+                nc.gpsimd.tensor_tensor(out=h[:], in0=up[:], in1=gate[:], op=ALU.mult)
+            else:
+                if with_lora:
+                    lora_out_scalar(e + 1, m, D_PASSES + c)
+                nc.vector.tensor_tensor(out=h[:], in0=up[:], in1=gate[:], op=ALU.mult)
             h_rows = out_0[e].rearrange("(p m) d -> p m d", m=TOKEN_TILES)
             nc.sync.dma_start(out=h_rows[:, m, BANK * c : BANK * (c + 1)], in_=h[:])
             if c == 0:
@@ -262,8 +267,8 @@ def tile_loralinearexpertswrapper_pa_e_kernel(
                 op0=ALU.mult,
                 op1=ALU.add,
             )
-            if with_lora:
-                lora_up_out(e + 1, m, c)
+            if with_lora and c == 0:
+                lora_out_vector(e + 1, m, D_PASSES + c)
 
         def transpose_h(e, m):
             h_ps = psum.tile([P, D_PASSES, 2, P], F32, tag="aux", bufs=5)
@@ -321,8 +326,8 @@ def tile_loralinearexpertswrapper_pa_e_kernel(
         for m in range(TOKEN_TILES):
             for c in range(D_PASSES):
                 lora_products(0, m, c)
-                lora_gate_out(0, m, c)
-                lora_up_out(0, m, c)
+                lora_out_scalar(0, m, c)
+                lora_out_vector(0, m, D_PASSES + c)
         transpose_b(1)
 
         for row in range(ROWS + 2):

@@ -25,6 +25,25 @@ PLANES_PER_TILE = 4
 LORA_SCALE = 2.0
 ROWS = E * TOKEN_TILES
 
+OPT = dict(
+    b_copy=("V", "S"),
+    b_copy_head=("V", "V"),
+    lora={(0, 0): "S", (0, 1): "V", (1, 0): "S", (1, 1): "S"},
+    mult={0: "G", 1: "V"},
+    rnd={0: "G", 1: "G"},
+    mult_last={0: "G", 1: "V"},
+    rnd_last={0: "G", 1: "G"},
+    lowd_copy="V",
+    lowd_copy_last="S",
+    hcopy="S",
+    base_bufs=3,
+    aux_bufs=5,
+    head=1,
+    tail=3,
+    split_b0=1,
+    end=dict(m=("G", "G", "G", "G"), r=("S", "S", "S")),
+)
+
 FLOPS = 2 * E * T * (2 * D) * H + 2 * E * T * (2 * D) * R + 2 * E * T * D * R
 
 
@@ -37,6 +56,7 @@ def tile_loralinearexpertswrapper_pa_e_kernel(
         work = ctx.enter_context(tc.tile_pool(name="work", bufs=2))
         psum = ctx.enter_context(tc.psum_pool(name="psum", bufs=1))
         ctx.enter_context(tc.manual_schedule())
+        AUX = OPT["aux_bufs"]
 
         x_sb = [keep.tile([P, TOKEN_TILES, H], BF16, name="x_sb%d" % e) for e in range(E)]
         low_sb = keep.tile([P, E, TOKEN_TILES, R], BF16, name="low_sb")
@@ -61,17 +81,25 @@ def tile_loralinearexpertswrapper_pa_e_kernel(
         nc.scalar.activation(out=warm[:, 1:2], in_=warm[:, 0:1], func=ACT.Silu)
 
         ident_f32 = keep.tile([P, P], F32, name="ident_f32")
-        make_identity(nc, ident_f32[:])
         ident_bf16 = keep.tile([P, P], BF16, name="ident_bf16")
-        make_identity(nc, ident_bf16[:])
+        if OPT["head"] == 0:
+            make_identity(nc, ident_f32[:])
+            make_identity(nc, ident_bf16[:])
+        else:
+            make_identity(nc, ident_bf16[:])
+            make_identity(nc, ident_f32[:])
 
         def load_x(e):
             nc.sync.dma_start(out=x_sb[e][:], in_=x[e].rearrange("(p m) k -> p m k", m=TOKEN_TILES))
 
-        def load_b(e):
-            nc.sync.dma_start(
-                out=b_sb[e][:], in_=B_gu[e].rearrange("(q p j) r -> p q j r", q=N_BANKS, p=P, j=PACK)
-            )
+        def load_b(e, parts=1):
+            rows = B_gu[e].rearrange("(q p j) r -> p q j r", q=N_BANKS, p=P, j=PACK)
+            step = N_BANKS // parts
+            for i in range(parts):
+                nc.sync.dma_start(out=b_sb[e][:, step * i : step * (i + 1)], in_=rows[:, step * i : step * (i + 1)])
+
+        def load_low():
+            nc.sync.dma_start(out=low_sb[:], in_=low_gu.rearrange("e (p m) r -> p e m r", m=TOKEN_TILES))
 
         def load_w_planes(b):
             for quadrant in range(4):
@@ -111,13 +139,22 @@ def tile_loralinearexpertswrapper_pa_e_kernel(
                     in_=W_gu_words[g].rearrange("p n t -> p (n t)").bitcast(I32),
                 )
 
-        load_x(0)
-        load_b(0)
-        nc.sync.dma_start(out=low_sb[:], in_=low_gu.rearrange("e (p m) r -> p e m r", m=TOKEN_TILES))
-        load_w_planes(0)
-        load_w_piece(0, 0)
-        load_b(1)
-        load_w_piece(0, 1)
+        if OPT["head"] == 0:
+            load_x(0)
+            load_b(0)
+            load_low()
+            load_w_planes(0)
+            load_w_piece(0, 0)
+            load_b(1)
+            load_w_piece(0, 1)
+        else:
+            load_low()
+            load_b(0, 2 if OPT["split_b0"] else 1)
+            load_x(0)
+            load_w_planes(0)
+            load_b(1)
+            load_w_piece(0, 0)
+            load_w_piece(0, 1)
         load_x(1)
         load_b(2)
         load_w_words(1)
@@ -141,13 +178,20 @@ def tile_loralinearexpertswrapper_pa_e_kernel(
         h_words = {}
         h_planes = {}
         low_d_sb = {}
+        low_d_banks = {}
+
+        def copy_out(engine, out, in_):
+            if engine == "S":
+                nc.scalar.copy(out=out, in_=in_)
+            else:
+                nc.vector.tensor_copy(out=out, in_=in_)
 
         def transpose_x(e):
             x_pairs = x_sb[e][:].rearrange("p m k -> p (m k)").bitcast(F32)
             grouped = work.tile([P, H_PASSES, TOKEN_TILES, P, PACK], BF16, tag="x_grouped", align_bytes=64)
             x_grouped[e] = grouped
             for kc in range(H_PASSES):
-                x_ps = psum.tile([P, TOKEN_TILES, 2, P], F32, tag="aux", bufs=5)
+                x_ps = psum.tile([P, TOKEN_TILES, 2, P], F32, tag="aux", bufs=AUX)
                 for m in range(TOKEN_TILES):
                     for u in range(2):
                         first = (H // 2) * m + (K_PASS // 2) * kc
@@ -173,22 +217,24 @@ def tile_loralinearexpertswrapper_pa_e_kernel(
                 in_=x_grouped[e][:].rearrange("p c m r t -> p (c m r t)"),
             )
 
-        def transpose_b(e):
+        def transpose_b(e, engines):
             flipped = work.tile([P, N_BANKS, PACK * P], BF16, tag="b_t")
             b_t[e] = flipped
             for half in range(2):
-                b_ps = psum.tile([P, 2, PACK, P], BF16, tag="aux", bufs=5)
+                b_ps = psum.tile([P, 2, PACK, P], BF16, tag="aux", bufs=AUX)
                 for i in range(2):
                     for j in range(PACK):
                         nc.tensor.transpose(b_ps[:, i, j, :], b_sb[e][:, 2 * half + i, j, :], ident_bf16[:])
-                nc.scalar.copy(
-                    out=flipped[:, 2 * half : 2 * half + 2, :], in_=b_ps[:].rearrange("r i j p -> r i (j p)")
+                copy_out(
+                    engines[half],
+                    flipped[:, 2 * half : 2 * half + 2, :],
+                    b_ps[:].rearrange("r i j p -> r i (j p)"),
                 )
 
         low_t = keep.tile([P, E, TOKEN_TILES, P], BF16, name="low_t")
 
         def transpose_low():
-            low_ps = psum.tile([P, E, TOKEN_TILES, P], BF16, tag="aux", bufs=5)
+            low_ps = psum.tile([P, E, TOKEN_TILES, P], BF16, tag="aux", bufs=AUX)
             for e in range(E):
                 for m in range(TOKEN_TILES):
                     nc.tensor.transpose(low_ps[:, e, m, :], low_sb[:, e, m, :], ident_bf16[:])
@@ -199,27 +245,27 @@ def tile_loralinearexpertswrapper_pa_e_kernel(
                 doubled = work.tile([P, TOKEN_TILES, N_BANKS, BANK], F32, tag="delta2")
                 delta2[e] = doubled
             for q in (c, D_PASSES + c):
-                delta_ps = psum.tile([P, BANK], F32, tag="aux", bufs=5)
+                delta_ps = psum.tile([P, BANK], F32, tag="aux", bufs=AUX)
                 nc.tensor.matmul(delta_ps[:], lhsT=low_t[:, e, m, :], rhs=b_t[e][:, q, :], start=True, stop=True)
                 delta_banks[(e, m, q)] = delta_ps
 
-        def lora_out_scalar(e, m, q):
-            nc.scalar.mul(
-                out=delta2[e][:, m, q, :].rearrange("r (p j) -> r p j", j=PACK),
-                in_=delta_banks[(e, m, q)][:].rearrange("r (j p) -> r p j", j=PACK),
-                mul=LORA_SCALE,
-            )
-
-        def lora_out_vector(e, m, q):
-            nc.vector.tensor_scalar_mul(
-                out=delta2[e][:, m, q, :].rearrange("r (p j) -> r p j", j=PACK),
-                in0=delta_banks[(e, m, q)][:].rearrange("r (j p) -> r p j", j=PACK),
-                scalar1=LORA_SCALE,
-            )
+        def lora_out(engine, e, m, q):
+            if engine == "S":
+                nc.scalar.mul(
+                    out=delta2[e][:, m, q, :].rearrange("r (p j) -> r p j", j=PACK),
+                    in_=delta_banks[(e, m, q)][:].rearrange("r (j p) -> r p j", j=PACK),
+                    mul=LORA_SCALE,
+                )
+            else:
+                nc.vector.tensor_scalar_mul(
+                    out=delta2[e][:, m, q, :].rearrange("r (p j) -> r p j", j=PACK),
+                    in0=delta_banks[(e, m, q)][:].rearrange("r (j p) -> r p j", j=PACK),
+                    scalar1=LORA_SCALE,
+                )
 
         def gate_up_passes(e, m, c):
             for half in range(2):
-                acc = psum.tile([P, BANK], F32, tag="base", bufs=3)
+                acc = psum.tile([P, BANK], F32, tag="base", bufs=OPT["base_bufs"])
                 for kc in range(H_PASSES):
                     g = H_PASSES * e + kc
                     offset = 4 * (g % PLANES_PER_TILE)
@@ -235,76 +281,139 @@ def tile_loralinearexpertswrapper_pa_e_kernel(
                     )
                 base_banks[(e, m, c, half)] = acc
 
+        def product(engine, out, in0, in1):
+            if engine == "G":
+                nc.gpsimd.tensor_tensor(out=out, in0=in0, in1=in1, op=ALU.mult)
+            else:
+                nc.vector.tensor_tensor(out=out, in0=in0, in1=in1, op=ALU.mult)
+
+        def rounding(engine, out, in_):
+            if engine == "G":
+                nc.gpsimd.tensor_scalar(out=out, in0=in_, scalar1=1.0, scalar2=0.0, op0=ALU.mult, op1=ALU.add)
+            elif engine == "S":
+                nc.scalar.copy(out=out, in_=in_)
+            else:
+                nc.vector.tensor_copy(out=out, in_=in_)
+
         def swiglu(e, m, c, with_lora):
+            last = e == E - 1
+            mult_engine = (OPT["mult_last"] if last else OPT["mult"])[c]
+            rnd_engine = (OPT["rnd_last"] if last else OPT["rnd"])[c]
+            final = OPT["tail"] >= 1 and last and m == TOKEN_TILES - 1 and c == D_PASSES - 1
             gate = work.tile([P, BANK], F32, tag="gate", bufs=3)
             nc.vector.tensor_tensor(
                 out=gate[:], in0=base_banks[(e, m, c, 0)][:], in1=delta2[e][:, m, c, :], op=ALU.add
             )
-            if with_lora:
-                lora_out_scalar(e + 1, m, c)
+            if with_lora and OPT["lora"][(c, 0)] == "S":
+                lora_out("S", e + 1, m, c)
             nc.scalar.activation(out=gate[:], in_=gate[:], func=ACT.Silu)
             up = work.tile([P, BANK], F32, tag="up", bufs=3)
             nc.vector.tensor_tensor(
                 out=up[:], in0=base_banks[(e, m, c, 1)][:], in1=delta2[e][:, m, D_PASSES + c, :], op=ALU.add
             )
-            h = work.tile([P, BANK], F32, tag="h", bufs=10)
-            if c == 0:
-                nc.gpsimd.tensor_tensor(out=h[:], in0=up[:], in1=gate[:], op=ALU.mult)
-            else:
-                if with_lora:
-                    lora_out_scalar(e + 1, m, D_PASSES + c)
-                nc.vector.tensor_tensor(out=h[:], in0=up[:], in1=gate[:], op=ALU.mult)
-            h_rows = out_0[e].rearrange("(p m) d -> p m d", m=TOKEN_TILES)
-            nc.sync.dma_start(out=h_rows[:, m, BANK * c : BANK * (c + 1)], in_=h[:])
+            if with_lora and OPT["lora"][(c, 0)] == "V":
+                lora_out("V", e + 1, m, c)
+            if with_lora and OPT["lora"][(c, 1)] == "S":
+                lora_out("S", e + 1, m, D_PASSES + c)
             if c == 0:
                 rounded = work.tile([P, D_PASSES, 2, P, 2], BF16, tag="h_bf16", bufs=3)
                 h_bf16[(e, m)] = rounded
-            nc.gpsimd.tensor_scalar(
-                out=h_bf16[(e, m)][:, c],
-                in0=h[:].rearrange("r (p u i) -> r u p i", u=2, i=2),
-                scalar1=1.0,
-                scalar2=0.0,
-                op0=ALU.mult,
-                op1=ALU.add,
-            )
-            if with_lora and c == 0:
-                lora_out_vector(e + 1, m, D_PASSES + c)
+            h = work.tile([P, BANK], F32, tag="h", bufs=10)
+            if final:
+                product(
+                    "V",
+                    h_bf16[(e, m)][:, c],
+                    up[:].rearrange("r (p u i) -> r u p i", u=2, i=2),
+                    gate[:].rearrange("r (p u i) -> r u p i", u=2, i=2),
+                )
+            product(mult_engine, h[:], up[:], gate[:])
+            h_rows = out_0[e].rearrange("(p m) d -> p m d", m=TOKEN_TILES)
+            nc.sync.dma_start(out=h_rows[:, m, BANK * c : BANK * (c + 1)], in_=h[:])
+            if not final:
+                rounding(rnd_engine, h_bf16[(e, m)][:, c], h[:].rearrange("r (p u i) -> r u p i", u=2, i=2))
+            if with_lora and OPT["lora"][(c, 1)] == "V":
+                lora_out("V", e + 1, m, D_PASSES + c)
 
-        def transpose_h(e, m):
-            h_ps = psum.tile([P, D_PASSES, 2, P], F32, tag="aux", bufs=5)
-            for c in range(D_PASSES):
+        gates = {}
+        ups = {}
+        hs = {}
+
+        def sums(e, m, c):
+            gate = work.tile([P, BANK], F32, tag="gate", bufs=3)
+            nc.vector.tensor_tensor(
+                out=gate[:], in0=base_banks[(e, m, c, 0)][:], in1=delta2[e][:, m, c, :], op=ALU.add
+            )
+            nc.scalar.activation(out=gate[:], in_=gate[:], func=ACT.Silu)
+            up = work.tile([P, BANK], F32, tag="up", bufs=3)
+            nc.vector.tensor_tensor(
+                out=up[:], in0=base_banks[(e, m, c, 1)][:], in1=delta2[e][:, m, D_PASSES + c, :], op=ALU.add
+            )
+            gates[(e, m, c)] = gate
+            ups[(e, m, c)] = up
+            if c == 0:
+                rounded = work.tile([P, D_PASSES, 2, P, 2], BF16, tag="h_bf16", bufs=3)
+                h_bf16[(e, m)] = rounded
+
+        def prod32(engine, e, m, c):
+            h = work.tile([P, BANK], F32, tag="h", bufs=10)
+            hs[(e, m, c)] = h
+            product(engine, h[:], ups[(e, m, c)][:], gates[(e, m, c)][:])
+            h_rows = out_0[e].rearrange("(p m) d -> p m d", m=TOKEN_TILES)
+            nc.sync.dma_start(out=h_rows[:, m, BANK * c : BANK * (c + 1)], in_=h[:])
+
+        def prod16(engine, e, m, c):
+            product(
+                engine,
+                h_bf16[(e, m)][:, c],
+                ups[(e, m, c)][:].rearrange("r (p u i) -> r u p i", u=2, i=2),
+                gates[(e, m, c)][:].rearrange("r (p u i) -> r u p i", u=2, i=2),
+            )
+
+        def rnd(engine, e, m, c):
+            rounding(engine, h_bf16[(e, m)][:, c], hs[(e, m, c)][:].rearrange("r (p u i) -> r u p i", u=2, i=2))
+
+        def transpose_h(e, m, pieces=(0, 1)):
+            if pieces[0] == 0:
+                grouped = work.tile([P, D_PASSES, P, PACK], BF16, tag="h_grouped", align_bytes=64)
+                h_grouped[(e, m)] = grouped
+            h_ps = psum.tile([P, D_PASSES, 2, P], F32, tag="aux", bufs=AUX)
+            for c in pieces:
                 for u in range(2):
                     nc.tensor.transpose(
                         h_ps[:, c, u, :],
                         h_bf16[(e, m)][:, c, u].rearrange("r p i -> r (p i)").bitcast(F32),
                         ident_f32[:],
                     )
-            grouped = work.tile([P, D_PASSES, P, PACK], BF16, tag="h_grouped", align_bytes=64)
-            h_grouped[(e, m)] = grouped
-            nc.scalar.copy(
-                out=grouped[:]
+            lo, hi = pieces[0], pieces[-1] + 1
+            copy_out(
+                OPT["hcopy"],
+                h_grouped[(e, m)][:, lo:hi]
                 .rearrange("p c r t -> p (c r t)")
                 .bitcast(F32)
-                .rearrange("p (c r u) -> p c r u", c=D_PASSES, u=2),
-                in_=h_ps[:].rearrange("p c u r -> p c r u"),
+                .rearrange("p (c r u) -> p c r u", c=hi - lo, u=2),
+                h_ps[:, lo:hi].rearrange("p c u r -> p c r u"),
             )
 
-        def quantise_h(e, m):
-            words = work.tile([P, D_PASSES, P], U32, tag="h_words", align_bytes=64)
-            planes = work.tile([P, D_PASSES, P], U8, tag="h_planes", align_bytes=64)
-            h_words[(e, m)] = words
-            h_planes[(e, m)] = planes
+        def quantise_h(e, m, pieces=(0, 1)):
+            if pieces[0] == 0:
+                words = work.tile([P, D_PASSES, P], U32, tag="h_words", align_bytes=64)
+                planes = work.tile([P, D_PASSES, P], U8, tag="h_planes", align_bytes=64)
+                h_words[(e, m)] = words
+                h_planes[(e, m)] = planes
+            lo, hi = pieces[0], pieces[-1] + 1
             nc.vector.quantize_mx(
-                out=words[:].rearrange("p c r -> p (c r)").bitcast(FP8X4),
-                scales=planes[:].rearrange("p c r -> p (c r)"),
-                in_=h_grouped[(e, m)][:].rearrange("p c r t -> p (c r t)"),
+                out=h_words[(e, m)][:, lo:hi].rearrange("p c r -> p (c r)").bitcast(FP8X4),
+                scales=h_planes[(e, m)][:, lo:hi].rearrange("p c r -> p (c r)"),
+                in_=h_grouped[(e, m)][:, lo:hi].rearrange("p c r t -> p (c r t)"),
             )
 
-        def low_rank(e, m):
-            low_d_ps = psum.tile([P, R], F32, tag="aux", bufs=5)
-            for c in range(D_PASSES):
+        def low_rank(e, m, pieces=(0, 1)):
+            if pieces[0] == 0:
+                low_d_ps = psum.tile([P, R], F32, tag="aux", bufs=AUX)
+                low_d_banks[(e, m)] = low_d_ps
+            for c in pieces:
                 nc.tensor.matmul_mx(
-                    out=low_d_ps[:],
+                    out=low_d_banks[(e, m)][:],
                     lhsT=h_words[(e, m)][:, c, :].bitcast(FP8X4),
                     lhsT_scale=h_planes[(e, m)][:, c, :],
                     rhs=a_words[:, D_PASSES * e + c, :].bitcast(FP8X4),
@@ -312,25 +421,39 @@ def tile_loralinearexpertswrapper_pa_e_kernel(
                     start=(c == 0),
                     stop=(c == D_PASSES - 1),
                 )
+            if pieces[-1] != D_PASSES - 1:
+                return
             if m == 0:
                 both_tiles = work.tile([P, TOKEN_TILES, R], F32, tag="low_d_sb")
                 low_d_sb[e] = both_tiles
-            nc.vector.tensor_copy(out=low_d_sb[e][:, m, :], in_=low_d_ps[:])
+            copy_out(
+                OPT["lowd_copy_last"] if e == E - 1 else OPT["lowd_copy"], low_d_sb[e][:, m, :], low_d_banks[(e, m)][:]
+            )
             if m == TOKEN_TILES - 1:
                 nc.sync.dma_start(out=out_1[e].rearrange("(p m) r -> p m r", m=TOKEN_TILES), in_=low_d_sb[e][:])
 
-        transpose_x(0)
-        quantise_x(0)
-        transpose_b(0)
-        transpose_low()
+        if OPT["head"] == 0:
+            transpose_x(0)
+            quantise_x(0)
+            transpose_b(0, OPT["b_copy_head"])
+            transpose_low()
+        else:
+            transpose_low()
+            transpose_b(0, OPT["b_copy_head"])
+            transpose_x(0)
+            quantise_x(0)
         for m in range(TOKEN_TILES):
             for c in range(D_PASSES):
                 lora_products(0, m, c)
-                lora_out_scalar(0, m, c)
-                lora_out_vector(0, m, D_PASSES + c)
-        transpose_b(1)
+                lora_out("S", 0, m, c)
+                lora_out("V", 0, m, D_PASSES + c)
+        transpose_b(1, OPT["b_copy_head"])
 
-        for row in range(ROWS + 2):
+        if OPT["tail"] == 3:
+            main_rows = ROWS - 2
+        else:
+            main_rows = ROWS + 2
+        for row in range(main_rows):
             e, m = divmod(row, TOKEN_TILES)
             for c in range(D_PASSES):
                 if row < ROWS:
@@ -339,15 +462,58 @@ def tile_loralinearexpertswrapper_pa_e_kernel(
                         lora_products(e + 1, m, c)
                     swiglu(e, m, c, e + 1 < E)
                 if c == 0:
-                    if row >= 2:
+                    if row >= 2 and not (OPT["tail"] >= 2 and row == ROWS + 1):
                         quantise_h((row - 2) // TOKEN_TILES, (row - 2) % TOKEN_TILES)
                     if m == 1 and e + 1 < E:
                         quantise_x(e + 1)
-            if row >= 2:
+                    if OPT["tail"] >= 2 and row == ROWS - 1:
+                        transpose_h(e, m, (0,))
+            if row >= 2 and not (OPT["tail"] >= 2 and row == ROWS + 1):
                 low_rank((row - 2) // TOKEN_TILES, (row - 2) % TOKEN_TILES)
             if m == 0 and e + 1 < E:
                 transpose_x(e + 1)
             if m == 1 and e + 2 < E:
-                transpose_b(e + 2)
+                transpose_b(e + 2, OPT["b_copy"])
             if 1 <= row <= ROWS:
-                transpose_h((row - 1) // TOKEN_TILES, (row - 1) % TOKEN_TILES)
+                if OPT["tail"] >= 2 and row == ROWS:
+                    quantise_h(E - 1, TOKEN_TILES - 1, (0,))
+                    transpose_h(E - 1, TOKEN_TILES - 1, (1,))
+                    low_rank(E - 1, TOKEN_TILES - 1, (0,))
+                    quantise_h(E - 1, TOKEN_TILES - 1, (1,))
+                    low_rank(E - 1, TOKEN_TILES - 1, (1,))
+                else:
+                    transpose_h((row - 1) // TOKEN_TILES, (row - 1) % TOKEN_TILES)
+
+        if OPT["tail"] == 3:
+            L = E - 1
+            EV = OPT["end"]
+            gate_up_passes(L, 0, 0)
+            sums(L, 0, 0)
+            prod32(EV["m"][0], L, 0, 0)
+            quantise_h(L - 1, 0)
+            gate_up_passes(L, 0, 1)
+            sums(L, 0, 1)
+            prod32(EV["m"][1], L, 0, 1)
+            rnd(EV["r"][0], L, 0, 0)
+            low_rank(L - 1, 0)
+            transpose_h(L - 1, 1)
+            gate_up_passes(L, 1, 0)
+            sums(L, 1, 0)
+            prod32(EV["m"][2], L, 1, 0)
+            rnd(EV["r"][1], L, 0, 1)
+            quantise_h(L - 1, 1)
+            gate_up_passes(L, 1, 1)
+            sums(L, 1, 1)
+            rnd(EV["r"][2], L, 1, 0)
+            low_rank(L - 1, 1)
+            transpose_h(L, 0)
+            transpose_h(L, 1, (0,))
+            prod16("V", L, 1, 1)
+            prod32(EV["m"][3], L, 1, 1)
+            quantise_h(L, 0)
+            transpose_h(L, 1, (1,))
+            quantise_h(L, 1, (0,))
+            low_rank(L, 0)
+            low_rank(L, 1, (0,))
+            quantise_h(L, 1, (1,))
+            low_rank(L, 1, (1,))

@@ -27,7 +27,7 @@ ROWS = E * TOKEN_TILES
 
 OPT = dict(
     b_copy=("V", "S"),
-    b_copy_head=("V", "V"),
+    b_copy_head=("S", "S"),
     lora={(0, 0): "S", (0, 1): "V", (1, 0): "S", (1, 1): "S"},
     mult={0: "G", 1: "V"},
     rnd={0: "G", 1: "G"},
@@ -38,10 +38,13 @@ OPT = dict(
     hcopy="S",
     base_bufs=3,
     aux_bufs=5,
-    head=1,
-    tail=3,
+    head=2,
+    tail=0,
     split_b0=1,
-    end=dict(m=("G", "G", "G", "G"), r=("S", "S", "S")),
+    qpos=2,
+    endp=2,
+    b1_copy=("V", "S"),
+    end=dict(m=("G", "G", "G", "V"), r=("S", "S", "S")),
 )
 
 FLOPS = 2 * E * T * (2 * D) * H + 2 * E * T * (2 * D) * R + 2 * E * T * D * R
@@ -240,14 +243,17 @@ def tile_loralinearexpertswrapper_pa_e_kernel(
                     nc.tensor.transpose(low_ps[:, e, m, :], low_sb[:, e, m, :], ident_bf16[:])
             nc.vector.tensor_copy(out=low_t[:], in_=low_ps[:])
 
-        def lora_products(e, m, c):
-            if m == 0 and c == 0:
+        def lora_product(e, m, q):
+            if e not in delta2:
                 doubled = work.tile([P, TOKEN_TILES, N_BANKS, BANK], F32, tag="delta2")
                 delta2[e] = doubled
+            delta_ps = psum.tile([P, BANK], F32, tag="aux", bufs=AUX)
+            nc.tensor.matmul(delta_ps[:], lhsT=low_t[:, e, m, :], rhs=b_t[e][:, q, :], start=True, stop=True)
+            delta_banks[(e, m, q)] = delta_ps
+
+        def lora_products(e, m, c):
             for q in (c, D_PASSES + c):
-                delta_ps = psum.tile([P, BANK], F32, tag="aux", bufs=AUX)
-                nc.tensor.matmul(delta_ps[:], lhsT=low_t[:, e, m, :], rhs=b_t[e][:, q, :], start=True, stop=True)
-                delta_banks[(e, m, q)] = delta_ps
+                lora_product(e, m, q)
 
         def lora_out(engine, e, m, q):
             if engine == "S":
@@ -338,11 +344,13 @@ def tile_loralinearexpertswrapper_pa_e_kernel(
         ups = {}
         hs = {}
 
-        def sums(e, m, c):
+        def sums(e, m, c, first_on_scalar=None):
             gate = work.tile([P, BANK], F32, tag="gate", bufs=3)
             nc.vector.tensor_tensor(
                 out=gate[:], in0=base_banks[(e, m, c, 0)][:], in1=delta2[e][:, m, c, :], op=ALU.add
             )
+            if first_on_scalar:
+                lora_out(*first_on_scalar)
             nc.scalar.activation(out=gate[:], in_=gate[:], func=ACT.Silu)
             up = work.tile([P, BANK], F32, tag="up", bufs=3)
             nc.vector.tensor_tensor(
@@ -432,60 +440,69 @@ def tile_loralinearexpertswrapper_pa_e_kernel(
             if m == TOKEN_TILES - 1:
                 nc.sync.dma_start(out=out_1[e].rearrange("(p m) r -> p m r", m=TOKEN_TILES), in_=low_d_sb[e][:])
 
-        if OPT["head"] == 0:
-            transpose_x(0)
-            quantise_x(0)
-            transpose_b(0, OPT["b_copy_head"])
-            transpose_low()
-        else:
-            transpose_low()
-            transpose_b(0, OPT["b_copy_head"])
-            transpose_x(0)
-            quantise_x(0)
-        for m in range(TOKEN_TILES):
-            for c in range(D_PASSES):
-                lora_products(0, m, c)
-                lora_out("S", 0, m, c)
-                lora_out("V", 0, m, D_PASSES + c)
-        transpose_b(1, OPT["b_copy_head"])
+        transpose_low()
+        transpose_b(0, ("V", "V"))
+        lora_product(0, 0, 0)
+        lora_product(0, 0, 1)
+        lora_out("S", 0, 0, 0)
+        lora_out("V", 0, 0, 1)
+        transpose_x(0)
+        lora_product(0, 0, 2)
+        lora_product(0, 0, 3)
+        lora_out("V", 0, 0, 2)
+        quantise_x(0)
+        lora_out("S", 0, 0, 3)
+        for q in range(N_BANKS):
+            lora_product(0, 1, q)
+            lora_out("V" if q % 2 == 0 else "S", 0, 1, q)
+        transpose_b(1, OPT["b1_copy"])
 
-        if OPT["tail"] == 3:
-            main_rows = ROWS - 2
-        else:
-            main_rows = ROWS + 2
-        for row in range(main_rows):
-            e, m = divmod(row, TOKEN_TILES)
-            for c in range(D_PASSES):
-                if row < ROWS:
-                    gate_up_passes(e, m, c)
-                    if e + 1 < E:
-                        lora_products(e + 1, m, c)
-                    swiglu(e, m, c, e + 1 < E)
-                if c == 0:
-                    if row >= 2 and not (OPT["tail"] >= 2 and row == ROWS + 1):
-                        quantise_h((row - 2) // TOKEN_TILES, (row - 2) % TOKEN_TILES)
-                    if m == 1 and e + 1 < E:
-                        quantise_x(e + 1)
-                    if OPT["tail"] >= 2 and row == ROWS - 1:
-                        transpose_h(e, m, (0,))
-            if row >= 2 and not (OPT["tail"] >= 2 and row == ROWS + 1):
-                low_rank((row - 2) // TOKEN_TILES, (row - 2) % TOKEN_TILES)
-            if m == 0 and e + 1 < E:
+        def em(row):
+            return row // TOKEN_TILES, row % TOKEN_TILES
+
+        QPOS = OPT["qpos"]
+        for row in range(ROWS - 2):
+            e, m = em(row)
+            gate_up_passes(e, m, 0)
+            lora_products(e + 1, m, 0)
+            sums(e, m, 0, ("S", e + 1, m, 0))
+            if QPOS == 2:
+                if row >= 2:
+                    quantise_h(*em(row - 2))
+                if m == 1:
+                    quantise_x(e + 1)
+            prod32("G", e, m, 0)
+            rnd("G", e, m, 0)
+            lora_out("V", e + 1, m, D_PASSES)
+            if QPOS == 0:
+                if row >= 2:
+                    quantise_h(*em(row - 2))
+                if m == 1:
+                    quantise_x(e + 1)
+            gate_up_passes(e, m, 1)
+            lora_products(e + 1, m, 1)
+            sums(e, m, 1, ("S", e + 1, m, 1))
+            lora_out("S", e + 1, m, D_PASSES + 1)
+            if QPOS == 1:
+                if row >= 2:
+                    quantise_h(*em(row - 2))
+                if m == 1:
+                    quantise_x(e + 1)
+            prod32("V", e, m, 1)
+            rnd("G", e, m, 1)
+            if QPOS != 1 and row >= 2:
+                low_rank(*em(row - 2))
+            if m == 0:
                 transpose_x(e + 1)
             if m == 1 and e + 2 < E:
                 transpose_b(e + 2, OPT["b_copy"])
-            if 1 <= row <= ROWS:
-                if OPT["tail"] >= 2 and row == ROWS:
-                    quantise_h(E - 1, TOKEN_TILES - 1, (0,))
-                    transpose_h(E - 1, TOKEN_TILES - 1, (1,))
-                    low_rank(E - 1, TOKEN_TILES - 1, (0,))
-                    quantise_h(E - 1, TOKEN_TILES - 1, (1,))
-                    low_rank(E - 1, TOKEN_TILES - 1, (1,))
-                else:
-                    transpose_h((row - 1) // TOKEN_TILES, (row - 1) % TOKEN_TILES)
+            if row >= 1:
+                transpose_h(*em(row - 1))
+            if QPOS == 1 and row >= 2:
+                low_rank(*em(row - 2))
 
-        if OPT["tail"] == 3:
-            L = E - 1
+        L = E - 1
+        if OPT["endp"] == 2:
             EV = OPT["end"]
             gate_up_passes(L, 0, 0)
             sums(L, 0, 0)
@@ -510,6 +527,37 @@ def tile_loralinearexpertswrapper_pa_e_kernel(
             transpose_h(L, 1, (0,))
             prod16("V", L, 1, 1)
             prod32(EV["m"][3], L, 1, 1)
+            quantise_h(L, 0)
+            transpose_h(L, 1, (1,))
+            quantise_h(L, 1, (0,))
+            low_rank(L, 0)
+            low_rank(L, 1, (0,))
+            quantise_h(L, 1, (1,))
+            low_rank(L, 1, (1,))
+        else:
+            gate_up_passes(L, 0, 0)
+            sums(L, 0, 0)
+            prod32("G", L, 0, 0)
+            gate_up_passes(L, 0, 1)
+            sums(L, 0, 1)
+            rnd("S", L, 0, 0)
+            quantise_h(L - 1, 0)
+            prod32("V", L, 0, 1)
+            transpose_h(L - 1, 1)
+            low_rank(L - 1, 0)
+            gate_up_passes(L, 1, 0)
+            sums(L, 1, 0)
+            prod32("G", L, 1, 0)
+            rnd("S", L, 0, 1)
+            gate_up_passes(L, 1, 1)
+            sums(L, 1, 1)
+            rnd("S", L, 1, 0)
+            transpose_h(L, 0)
+            transpose_h(L, 1, (0,))
+            prod32("V", L, 1, 1)
+            rnd("S", L, 1, 1)
+            quantise_h(L - 1, 1)
+            low_rank(L - 1, 1)
             quantise_h(L, 0)
             transpose_h(L, 1, (1,))
             quantise_h(L, 1, (0,))

@@ -42,6 +42,11 @@ OPT = dict(
     tail=0,
     split_b0=1,
     qpos=2,
+    early_b=1,
+    h_bufs=10,
+    silu_first=0,
+    one_ring=0,
+    warm=0,
     endp=2,
     b1_copy=("V", "S"),
     end=dict(m=("G", "G", "G", "V"), r=("S", "S", "S")),
@@ -74,6 +79,13 @@ def tile_loralinearexpertswrapper_pa_e_kernel(
         ]
         a_words = keep.tile([P, E * D_PASSES, R], U32, name="a_words", align_bytes=64)
         a_planes = keep.tile([P, E * D_PASSES, R], U8, name="a_planes", align_bytes=64)
+
+        if OPT["warm"]:
+            warm_bf = keep.tile([P, BANK], BF16, name="warm_bf")
+            nc.vector.memset(warm_bf[:], 0.0)
+            for i in range(OPT["warm"]):
+                warm_ps = psum.tile([P, BANK], F32, tag=("aux" if OPT["one_ring"] else "base"), bufs=(AUX if OPT["one_ring"] else OPT["base_bufs"]))
+                nc.tensor.matmul(warm_ps[:], lhsT=warm_bf[:, 0:P], rhs=warm_bf[:], start=True, stop=True)
 
         for plane_tile in w_planes:
             nc.vector.memset(plane_tile[:].bitcast(I32), 0)
@@ -271,7 +283,7 @@ def tile_loralinearexpertswrapper_pa_e_kernel(
 
         def gate_up_passes(e, m, c):
             for half in range(2):
-                acc = psum.tile([P, BANK], F32, tag="base", bufs=OPT["base_bufs"])
+                acc = psum.tile([P, BANK], F32, tag=("aux" if OPT["one_ring"] else "base"), bufs=(AUX if OPT["one_ring"] else OPT["base_bufs"]))
                 for kc in range(H_PASSES):
                     g = H_PASSES * e + kc
                     offset = 4 * (g % PLANES_PER_TILE)
@@ -324,7 +336,7 @@ def tile_loralinearexpertswrapper_pa_e_kernel(
             if c == 0:
                 rounded = work.tile([P, D_PASSES, 2, P, 2], BF16, tag="h_bf16", bufs=3)
                 h_bf16[(e, m)] = rounded
-            h = work.tile([P, BANK], F32, tag="h", bufs=10)
+            h = work.tile([P, BANK], F32, tag="h", bufs=OPT["h_bufs"])
             if final:
                 product(
                     "V",
@@ -349,9 +361,11 @@ def tile_loralinearexpertswrapper_pa_e_kernel(
             nc.vector.tensor_tensor(
                 out=gate[:], in0=base_banks[(e, m, c, 0)][:], in1=delta2[e][:, m, c, :], op=ALU.add
             )
-            if first_on_scalar:
+            if first_on_scalar and not OPT["silu_first"]:
                 lora_out(*first_on_scalar)
             nc.scalar.activation(out=gate[:], in_=gate[:], func=ACT.Silu)
+            if first_on_scalar and OPT["silu_first"]:
+                lora_out(*first_on_scalar)
             up = work.tile([P, BANK], F32, tag="up", bufs=3)
             nc.vector.tensor_tensor(
                 out=up[:], in0=base_banks[(e, m, c, 1)][:], in1=delta2[e][:, m, D_PASSES + c, :], op=ALU.add
@@ -363,7 +377,7 @@ def tile_loralinearexpertswrapper_pa_e_kernel(
                 h_bf16[(e, m)] = rounded
 
         def prod32(engine, e, m, c):
-            h = work.tile([P, BANK], F32, tag="h", bufs=10)
+            h = work.tile([P, BANK], F32, tag="h", bufs=OPT["h_bufs"])
             hs[(e, m, c)] = h
             product(engine, h[:], ups[(e, m, c)][:], gates[(e, m, c)][:])
             h_rows = out_0[e].rearrange("(p m) d -> p m d", m=TOKEN_TILES)
@@ -488,14 +502,18 @@ def tile_loralinearexpertswrapper_pa_e_kernel(
                     quantise_h(*em(row - 2))
                 if m == 1:
                     quantise_x(e + 1)
-            prod32("V", e, m, 1)
-            rnd("G", e, m, 1)
+            if not OPT["early_b"]:
+                prod32("V", e, m, 1)
+                rnd("G", e, m, 1)
             if QPOS != 1 and row >= 2:
                 low_rank(*em(row - 2))
             if m == 0:
                 transpose_x(e + 1)
             if m == 1 and e + 2 < E:
                 transpose_b(e + 2, OPT["b_copy"])
+            if OPT["early_b"]:
+                prod32("V", e, m, 1)
+                rnd("G", e, m, 1)
             if row >= 1:
                 transpose_h(*em(row - 1))
             if QPOS == 1 and row >= 2:

@@ -42,6 +42,9 @@ OPT = dict(
     tail=0,
     split_b0=1,
     qpos=2,
+    ls_odd=1,
+    ls_from=5,
+    g_from=5,
     early_b=1,
     h_bufs=10,
     silu_first=0,
@@ -487,7 +490,7 @@ def tile_loralinearexpertswrapper_pa_e_kernel(
                     quantise_x(e + 1)
             prod32("G", e, m, 0)
             rnd("G", e, m, 0)
-            lora_out("V", e + 1, m, D_PASSES)
+            lora_out("S" if (row >= OPT["ls_from"] or (OPT["ls_odd"] and m == 1)) else "V", e + 1, m, D_PASSES)
             if QPOS == 0:
                 if row >= 2:
                     quantise_h(*em(row - 2))
@@ -512,7 +515,7 @@ def tile_loralinearexpertswrapper_pa_e_kernel(
             if m == 1 and e + 2 < E:
                 transpose_b(e + 2, OPT["b_copy"])
             if OPT["early_b"]:
-                prod32("V", e, m, 1)
+                prod32("G" if row >= OPT["g_from"] else "V", e, m, 1)
                 rnd("G", e, m, 1)
             if row >= 1:
                 transpose_h(*em(row - 1))

@@ -37,18 +37,19 @@ OPT = dict(
     lowd_copy_last="S",
     hcopy="S",
     base_bufs=3,
-    aux_bufs=5,
+    aux_bufs=8,
     head=2,
     tail=0,
     split_b0=1,
     qpos=2,
+    l11="S",
     ls_odd=1,
     ls_from=5,
     g_from=5,
     early_b=1,
     h_bufs=10,
     silu_first=0,
-    one_ring=0,
+    one_ring=1,
     warm=0,
     endp=2,
     b1_copy=("V", "S"),
@@ -499,7 +500,7 @@ def tile_loralinearexpertswrapper_pa_e_kernel(
             gate_up_passes(e, m, 1)
             lora_products(e + 1, m, 1)
             sums(e, m, 1, ("S", e + 1, m, 1))
-            lora_out("S", e + 1, m, D_PASSES + 1)
+            lora_out(OPT["l11"], e + 1, m, D_PASSES + 1)
             if QPOS == 1:
                 if row >= 2:
                     quantise_h(*em(row - 2))

@@ -42,6 +42,8 @@ OPT = dict(
     tail=0,
     split_b0=1,
     qpos=2,
+    b4=1,
+    s_store=0,
     l11="S",
     ls_odd=1,
     ls_from=5,
@@ -239,7 +241,12 @@ def tile_loralinearexpertswrapper_pa_e_kernel(
         def transpose_b(e, engines):
             flipped = work.tile([P, N_BANKS, PACK * P], BF16, tag="b_t")
             b_t[e] = flipped
-            for half in range(2):
+            for q in range(N_BANKS if OPT["b4"] else 0):
+                b_ps = psum.tile([P, PACK, P], BF16, tag="aux", bufs=AUX)
+                for j in range(PACK):
+                    nc.tensor.transpose(b_ps[:, j, :], b_sb[e][:, q, j, :], ident_bf16[:])
+                copy_out(engines[q // 2], flipped[:, q, :], b_ps[:].rearrange("r j p -> r (j p)"))
+            for half in range(0 if OPT["b4"] else 2):
                 b_ps = psum.tile([P, 2, PACK, P], BF16, tag="aux", bufs=AUX)
                 for i in range(2):
                     for j in range(PACK):
@@ -456,7 +463,10 @@ def tile_loralinearexpertswrapper_pa_e_kernel(
                 OPT["lowd_copy_last"] if e == E - 1 else OPT["lowd_copy"], low_d_sb[e][:, m, :], low_d_banks[(e, m)][:]
             )
             if m == TOKEN_TILES - 1:
-                nc.sync.dma_start(out=out_1[e].rearrange("(p m) r -> p m r", m=TOKEN_TILES), in_=low_d_sb[e][:])
+                if OPT["s_store"] and e == E - 1:
+                    nc.scalar.dma_start(out=out_1[e].rearrange("(p m) r -> p m r", m=TOKEN_TILES), in_=low_d_sb[e][:])
+                else:
+                    nc.sync.dma_start(out=out_1[e].rearrange("(p m) r -> p m r", m=TOKEN_TILES), in_=low_d_sb[e][:])
 
         transpose_low()
         transpose_b(0, ("V", "V"))

from contextlib import ExitStack

import concourse.mybir as mybir
from concourse.masks import make_identity

F32 = mybir.dt.float32
BF16 = mybir.dt.bfloat16
I32 = mybir.dt.int32
U32 = mybir.dt.uint32
U8 = mybir.dt.uint8
FP8X4 = mybir.dt.float8_e4m3fn_x4
ALU = mybir.AluOpType
ACT = mybir.ActivationFunctionType

E, T, H, D, R = 4, 256, 1024, 1024, 128
P = 128
PACK = 4
K_PASS = P * PACK
BANK = 512
TOKEN_TILES = T // P
H_PASSES = H // K_PASS
D_PASSES = D // K_PASS
N_BANKS = 2 * D // BANK
PLANES_PER_TILE = 4
LORA_SCALE = 2.0
ROWS = E * TOKEN_TILES

OPT = dict(
    b_copy=("V", "S"),
    b_copy_head=("S", "S"),
    lora={(0, 0): "S", (0, 1): "V", (1, 0): "S", (1, 1): "S"},
    mult={0: "G", 1: "V"},
    rnd={0: "G", 1: "G"},
    mult_last={0: "G", 1: "V"},
    rnd_last={0: "G", 1: "G"},
    lowd_copy="V",
    lowd_copy_last="S",
    hcopy="S",
    base_bufs=3,
    aux_bufs=8,
    head=2,
    tail=0,
    split_b0=1,
    qpos=2,
    b4=1,
    s_store=0,
    l11="S",
    ls_odd=1,
    ls_from=5,
    g_from=5,
    early_b=1,
    h_bufs=10,
    silu_first=0,
    one_ring=1,
    warm=0,
    endp=2,
    b1_copy=("V", "S"),
    end=dict(m=("G", "G", "G", "V"), r=("S", "S", "S")),
)

FLOPS = 2 * E * T * (2 * D) * H + 2 * E * T * (2 * D) * R + 2 * E * T * D * R


def tile_loralinearexpertswrapper_pa_e_kernel(
    tc, x, low_gu, W_gu_words, W_gu_scales, B_gu, A_d_words, A_d_scales, out_0, out_1
):
    nc = tc.nc
    with ExitStack() as ctx:
        keep = ctx.enter_context(tc.tile_pool(name="keep", bufs=1))
        work = ctx.enter_context(tc.tile_pool(name="work", bufs=2))
        psum = ctx.enter_context(tc.psum_pool(name="psum", bufs=1))
        ctx.enter_context(tc.manual_schedule())
        AUX = OPT["aux_bufs"]

        x_sb = [keep.tile([P, TOKEN_TILES, H], BF16, name="x_sb%d" % e) for e in range(E)]
        low_sb = keep.tile([P, E, TOKEN_TILES, R], BF16, name="low_sb")
        b_sb = [keep.tile([P, N_BANKS, PACK, R], BF16, name="b_sb%d" % e) for e in range(E)]
        w_words = [
            keep.tile([P, 2, D_PASSES, BANK], U32, name="w_words%d" % g, align_bytes=64)
            for g in range(E * H_PASSES)
        ]
        w_planes = [
            keep.tile([P, 2 * D], U8, name="w_planes%d" % b, align_bytes=64)
            for b in range(E * H_PASSES // PLANES_PER_TILE)
        ]
        a_words = keep.tile([P, E * D_PASSES, R], U32, name="a_words", align_bytes=64)
        a_planes = keep.tile([P, E * D_PASSES, R], U8, name="a_planes", align_bytes=64)

        if OPT["warm"]:
            warm_bf = keep.tile([P, BANK], BF16, name="warm_bf")
            nc.vector.memset(warm_bf[:], 0.0)
            for i in range(OPT["warm"]):
                warm_ps = psum.tile([P, BANK], F32, tag=("aux" if OPT["one_ring"] else "base"), bufs=(AUX if OPT["one_ring"] else OPT["base_bufs"]))
                nc.tensor.matmul(warm_ps[:], lhsT=warm_bf[:, 0:P], rhs=warm_bf[:], start=True, stop=True)

        for plane_tile in w_planes:
            nc.vector.memset(plane_tile[:].bitcast(I32), 0)
        nc.vector.memset(a_planes[:].rearrange("p g n -> p (g n)").bitcast(I32), 0)

        warm = keep.tile([P, 2], F32, name="warm")
        nc.vector.memset(warm[:, 0:1], 0.0)
        nc.scalar.activation(out=warm[:, 1:2], in_=warm[:, 0:1], func=ACT.Silu)

        ident_f32 = keep.tile([P, P], F32, name="ident_f32")
        ident_bf16 = keep.tile([P, P], BF16, name="ident_bf16")
        if OPT["head"] == 0:
            make_identity(nc, ident_f32[:])
            make_identity(nc, ident_bf16[:])
        else:
            make_identity(nc, ident_bf16[:])
            make_identity(nc, ident_f32[:])

        def load_x(e):
            nc.sync.dma_start(out=x_sb[e][:], in_=x[e].rearrange("(p m) k -> p m k", m=TOKEN_TILES))

        def load_b(e, parts=1):
            rows = B_gu[e].rearrange("(q p j) r -> p q j r", q=N_BANKS, p=P, j=PACK)
            step = N_BANKS // parts
            for i in range(parts):
                nc.sync.dma_start(out=b_sb[e][:, step * i : step * (i + 1)], in_=rows[:, step * i : step * (i + 1)])

        def load_low():
            nc.sync.dma_start(out=low_sb[:], in_=low_gu.rearrange("e (p m) r -> p e m r", m=TOKEN_TILES))

        def load_w_planes(b):
            for quadrant in range(4):
                nc.sync.dma_start(
                    out=w_planes[b][32 * quadrant : 32 * quadrant + 16, :].bitcast(I32),
                    in_=W_gu_scales[
                        PLANES_PER_TILE * b : PLANES_PER_TILE * (b + 1), 4 * quadrant : 4 * quadrant + 4, :
                    ].bitcast(I32),
                )

        def load_a():
            nc.sync.dma_start(
                out=a_words[:].bitcast(I32), in_=A_d_words.rearrange("g p n t -> p g (n t)").bitcast(I32)
            )
            for quadrant in range(4):
                nc.sync.dma_start(
                    out=a_planes[32 * quadrant : 32 * quadrant + 4, :, :].bitcast(I32),
                    in_=A_d_scales[:, 4 * quadrant : 4 * quadrant + 4, :].rearrange("g r n -> r g n").bitcast(I32),
                )

        def load_w_piece(e, c):
            for kc in range(H_PASSES):
                g = H_PASSES * e + kc
                pieces = (
                    W_gu_words[g]
                    .rearrange("p n t -> p (n t)")
                    .bitcast(I32)
                    .rearrange("p (half c n) -> p half c n", half=2, c=D_PASSES)
                )
                nc.sync.dma_start(out=w_words[g][:, :, c, :].bitcast(I32), in_=pieces[:, :, c, :])

        def load_w_words(e):
            for kc in range(H_PASSES):
                g = H_PASSES * e + kc
                nc.sync.dma_start(
                    out=w_words[g][:].rearrange("p half c n -> p (half c n)").bitcast(I32),
                    in_=W_gu_words[g].rearrange("p n t -> p (n t)").bitcast(I32),
                )

        if OPT["head"] == 0:
            load_x(0)
            load_b(0)
            load_low()
            load_w_planes(0)
            load_w_piece(0, 0)
            load_b(1)
            load_w_piece(0, 1)
        else:
            load_low()
            load_b(0, 2 if OPT["split_b0"] else 1)
            load_x(0)
            load_w_planes(0)
            load_b(1)
            load_w_piece(0, 0)
            load_w_piece(0, 1)
        load_x(1)
        load_b(2)
        load_w_words(1)
        load_a()
        load_x(2)
        load_b(3)
        load_w_planes(1)
        load_w_words(2)
        load_x(3)
        load_w_words(3)

        x_grouped = {}
        x_words = {}
        x_planes = {}
        b_t = {}
        delta2 = {}
        delta_banks = {}
        base_banks = {}
        h_bf16 = {}
        h_grouped = {}
        h_words = {}
        h_planes = {}
        low_d_sb = {}
        low_d_banks = {}

        def copy_out(engine, out, in_):
            if engine == "S":
                nc.scalar.copy(out=out, in_=in_)
            else:
                nc.vector.tensor_copy(out=out, in_=in_)

        def transpose_x(e):
            x_pairs = x_sb[e][:].rearrange("p m k -> p (m k)").bitcast(F32)
            grouped = work.tile([P, H_PASSES, TOKEN_TILES, P, PACK], BF16, tag="x_grouped", align_bytes=64)
            x_grouped[e] = grouped
            for kc in range(H_PASSES):
                x_ps = psum.tile([P, TOKEN_TILES, 2, P], F32, tag="aux", bufs=AUX)
                for m in range(TOKEN_TILES):
                    for u in range(2):
                        first = (H // 2) * m + (K_PASS // 2) * kc
                        nc.tensor.transpose(
                            x_ps[:, m, u, :], x_pairs[:, first + u : first + K_PASS // 2 : 2], ident_f32[:]
                        )
                nc.scalar.copy(
                    out=grouped[:, kc]
                    .rearrange("p m r t -> p (m r t)")
                    .bitcast(F32)
                    .rearrange("p (m r u) -> p m r u", m=TOKEN_TILES, u=2),
                    in_=x_ps[:].rearrange("p m u r -> p m r u"),
                )

        def quantise_x(e):
            words = work.tile([P, H_PASSES, TOKEN_TILES, P], U32, tag="x_words", align_bytes=64)
            planes = work.tile([P, H_PASSES, TOKEN_TILES, P], U8, tag="x_planes", align_bytes=64)
            x_words[e] = words
            x_planes[e] = planes
            nc.vector.quantize_mx(
                out=words[:].rearrange("p c m r -> p (c m r)").bitcast(FP8X4),
                scales=planes[:].rearrange("p c m r -> p (c m r)"),
                in_=x_grouped[e][:].rearrange("p c m r t -> p (c m r t)"),
            )

        def transpose_b(e, engines):
            flipped = work.tile([P, N_BANKS, PACK * P], BF16, tag="b_t")
            b_t[e] = flipped
            for q in range(N_BANKS if OPT["b4"] else 0):
                b_ps = psum.tile([P, PACK, P], BF16, tag="aux", bufs=AUX)
                for j in range(PACK):
                    nc.tensor.transpose(b_ps[:, j, :], b_sb[e][:, q, j, :], ident_bf16[:])
                copy_out(engines[q // 2], flipped[:, q, :], b_ps[:].rearrange("r j p -> r (j p)"))
            for half in range(0 if OPT["b4"] else 2):
                b_ps = psum.tile([P, 2, PACK, P], BF16, tag="aux", bufs=AUX)
                for i in range(2):
                    for j in range(PACK):
                        nc.tensor.transpose(b_ps[:, i, j, :], b_sb[e][:, 2 * half + i, j, :], ident_bf16[:])
                copy_out(
                    engines[half],
                    flipped[:, 2 * half : 2 * half + 2, :],
                    b_ps[:].rearrange("r i j p -> r i (j p)"),
                )

        low_t = keep.tile([P, E, TOKEN_TILES, P], BF16, name="low_t")

        def transpose_low():
            low_ps = psum.tile([P, E, TOKEN_TILES, P], BF16, tag="aux", bufs=AUX)
            for e in range(E):
                for m in range(TOKEN_TILES):
                    nc.tensor.transpose(low_ps[:, e, m, :], low_sb[:, e, m, :], ident_bf16[:])
            nc.vector.tensor_copy(out=low_t[:], in_=low_ps[:])

        def lora_product(e, m, q):
            if e not in delta2:
                doubled = work.tile([P, TOKEN_TILES, N_BANKS, BANK], F32, tag="delta2")
                delta2[e] = doubled
            delta_ps = psum.tile([P, BANK], F32, tag="aux", bufs=AUX)
            nc.tensor.matmul(delta_ps[:], lhsT=low_t[:, e, m, :], rhs=b_t[e][:, q, :], start=True, stop=True)
            delta_banks[(e, m, q)] = delta_ps

        def lora_products(e, m, c):
            for q in (c, D_PASSES + c):
                lora_product(e, m, q)

        def lora_out(engine, e, m, q):
            if engine == "S":
                nc.scalar.mul(
                    out=delta2[e][:, m, q, :].rearrange("r (p j) -> r p j", j=PACK),
                    in_=delta_banks[(e, m, q)][:].rearrange("r (j p) -> r p j", j=PACK),
                    mul=LORA_SCALE,
                )
            else:
                nc.vector.tensor_scalar_mul(
                    out=delta2[e][:, m, q, :].rearrange("r (p j) -> r p j", j=PACK),
                    in0=delta_banks[(e, m, q)][:].rearrange("r (j p) -> r p j", j=PACK),
                    scalar1=LORA_SCALE,
                )

        def gate_up_passes(e, m, c):
            for half in range(2):
                acc = psum.tile([P, BANK], F32, tag=("aux" if OPT["one_ring"] else "base"), bufs=(AUX if OPT["one_ring"] else OPT["base_bufs"]))
                for kc in range(H_PASSES):
                    g = H_PASSES * e + kc
                    offset = 4 * (g % PLANES_PER_TILE)
                    first = D * half + BANK * c
                    nc.tensor.matmul_mx(
                        out=acc[:],
                        lhsT=x_words[e][:, kc, m, :].bitcast(FP8X4),
                        lhsT_scale=x_planes[e][:, kc, m, :],
                        rhs=w_words[g][:, half, c, :].bitcast(FP8X4),
                        rhs_scale=w_planes[g // PLANES_PER_TILE][offset:P, first : first + BANK],
                        start=(kc == 0),
                        stop=(kc == H_PASSES - 1),
                    )
                base_banks[(e, m, c, half)] = acc

        def product(engine, out, in0, in1):
            if engine == "G":
                nc.gpsimd.tensor_tensor(out=out, in0=in0, in1=in1, op=ALU.mult)
            else:
                nc.vector.tensor_tensor(out=out, in0=in0, in1=in1, op=ALU.mult)

        def rounding(engine, out, in_):
            if engine == "G":
                nc.gpsimd.tensor_scalar(out=out, in0=in_, scalar1=1.0, scalar2=0.0, op0=ALU.mult, op1=ALU.add)
            elif engine == "S":
                nc.scalar.copy(out=out, in_=in_)
            else:
                nc.vector.tensor_copy(out=out, in_=in_)

        def swiglu(e, m, c, with_lora):
            last = e == E - 1
            mult_engine = (OPT["mult_last"] if last else OPT["mult"])[c]
            rnd_engine = (OPT["rnd_last"] if last else OPT["rnd"])[c]
            final = OPT["tail"] >= 1 and last and m == TOKEN_TILES - 1 and c == D_PASSES - 1
            gate = work.tile([P, BANK], F32, tag="gate", bufs=3)
            nc.vector.tensor_tensor(
                out=gate[:], in0=base_banks[(e, m, c, 0)][:], in1=delta2[e][:, m, c, :], op=ALU.add
            )
            if with_lora and OPT["lora"][(c, 0)] == "S":
                lora_out("S", e + 1, m, c)
            nc.scalar.activation(out=gate[:], in_=gate[:], func=ACT.Silu)
            up = work.tile([P, BANK], F32, tag="up", bufs=3)
            nc.vector.tensor_tensor(
                out=up[:], in0=base_banks[(e, m, c, 1)][:], in1=delta2[e][:, m, D_PASSES + c, :], op=ALU.add
            )
            if with_lora and OPT["lora"][(c, 0)] == "V":
                lora_out("V", e + 1, m, c)
            if with_lora and OPT["lora"][(c, 1)] == "S":
                lora_out("S", e + 1, m, D_PASSES + c)
            if c == 0:
                rounded = work.tile([P, D_PASSES, 2, P, 2], BF16, tag="h_bf16", bufs=3)
                h_bf16[(e, m)] = rounded
            h = work.tile([P, BANK], F32, tag="h", bufs=OPT["h_bufs"])
            if final:
                product(
                    "V",
                    h_bf16[(e, m)][:, c],
                    up[:].rearrange("r (p u i) -> r u p i", u=2, i=2),
                    gate[:].rearrange("r (p u i) -> r u p i", u=2, i=2),
                )
            product(mult_engine, h[:], up[:], gate[:])
            h_rows = out_0[e].rearrange("(p m) d -> p m d", m=TOKEN_TILES)
            nc.sync.dma_start(out=h_rows[:, m, BANK * c : BANK * (c + 1)], in_=h[:])
            if not final:
                rounding(rnd_engine, h_bf16[(e, m)][:, c], h[:].rearrange("r (p u i) -> r u p i", u=2, i=2))
            if with_lora and OPT["lora"][(c, 1)] == "V":
                lora_out("V", e + 1, m, D_PASSES + c)

        gates = {}
        ups = {}
        hs = {}

        def sums(e, m, c, first_on_scalar=None):
            gate = work.tile([P, BANK], F32, tag="gate", bufs=3)
            nc.vector.tensor_tensor(
                out=gate[:], in0=base_banks[(e, m, c, 0)][:], in1=delta2[e][:, m, c, :], op=ALU.add
            )
            if first_on_scalar and not OPT["silu_first"]:
                lora_out(*first_on_scalar)
            nc.scalar.activation(out=gate[:], in_=gate[:], func=ACT.Silu)
            if first_on_scalar and OPT["silu_first"]:
                lora_out(*first_on_scalar)
            up = work.tile([P, BANK], F32, tag="up", bufs=3)
            nc.vector.tensor_tensor(
                out=up[:], in0=base_banks[(e, m, c, 1)][:], in1=delta2[e][:, m, D_PASSES + c, :], op=ALU.add
            )
            gates[(e, m, c)] = gate
            ups[(e, m, c)] = up
            if c == 0:
                rounded = work.tile([P, D_PASSES, 2, P, 2], BF16, tag="h_bf16", bufs=3)
                h_bf16[(e, m)] = rounded

        def prod32(engine, e, m, c):
            h = work.tile([P, BANK], F32, tag="h", bufs=OPT["h_bufs"])
            hs[(e, m, c)] = h
            product(engine, h[:], ups[(e, m, c)][:], gates[(e, m, c)][:])
            h_rows = out_0[e].rearrange("(p m) d -> p m d", m=TOKEN_TILES)
            nc.sync.dma_start(out=h_rows[:, m, BANK * c : BANK * (c + 1)], in_=h[:])

        def prod16(engine, e, m, c):
            product(
                engine,
                h_bf16[(e, m)][:, c],
                ups[(e, m, c)][:].rearrange("r (p u i) -> r u p i", u=2, i=2),
                gates[(e, m, c)][:].rearrange("r (p u i) -> r u p i", u=2, i=2),
            )

        def rnd(engine, e, m, c):
            rounding(engine, h_bf16[(e, m)][:, c], hs[(e, m, c)][:].rearrange("r (p u i) -> r u p i", u=2, i=2))

        def transpose_h(e, m, pieces=(0, 1)):
            if pieces[0] == 0:
                grouped = work.tile([P, D_PASSES, P, PACK], BF16, tag="h_grouped", align_bytes=64)
                h_grouped[(e, m)] = grouped
            h_ps = psum.tile([P, D_PASSES, 2, P], F32, tag="aux", bufs=AUX)
            for c in pieces:
                for u in range(2):
                    nc.tensor.transpose(
                        h_ps[:, c, u, :],
                        h_bf16[(e, m)][:, c, u].rearrange("r p i -> r (p i)").bitcast(F32),
                        ident_f32[:],
                    )
            lo, hi = pieces[0], pieces[-1] + 1
            copy_out(
                OPT["hcopy"],
                h_grouped[(e, m)][:, lo:hi]
                .rearrange("p c r t -> p (c r t)")
                .bitcast(F32)
                .rearrange("p (c r u) -> p c r u", c=hi - lo, u=2),
                h_ps[:, lo:hi].rearrange("p c u r -> p c r u"),
            )

        def quantise_h(e, m, pieces=(0, 1)):
            if pieces[0] == 0:
                words = work.tile([P, D_PASSES, P], U32, tag="h_words", align_bytes=64)
                planes = work.tile([P, D_PASSES, P], U8, tag="h_planes", align_bytes=64)
                h_words[(e, m)] = words
                h_planes[(e, m)] = planes
            lo, hi = pieces[0], pieces[-1] + 1
            nc.vector.quantize_mx(
                out=h_words[(e, m)][:, lo:hi].rearrange("p c r -> p (c r)").bitcast(FP8X4),
                scales=h_planes[(e, m)][:, lo:hi].rearrange("p c r -> p (c r)"),
                in_=h_grouped[(e, m)][:, lo:hi].rearrange("p c r t -> p (c r t)"),
            )

        def low_rank(e, m, pieces=(0, 1)):
            if pieces[0] == 0:
                low_d_ps = psum.tile([P, R], F32, tag="aux", bufs=AUX)
                low_d_banks[(e, m)] = low_d_ps
            for c in pieces:
                nc.tensor.matmul_mx(
                    out=low_d_banks[(e, m)][:],
                    lhsT=h_words[(e, m)][:, c, :].bitcast(FP8X4),
                    lhsT_scale=h_planes[(e, m)][:, c, :],
                    rhs=a_words[:, D_PASSES * e + c, :].bitcast(FP8X4),
                    rhs_scale=a_planes[:, D_PASSES * e + c, :],
                    start=(c == 0),
                    stop=(c == D_PASSES - 1),
                )
            if pieces[-1] != D_PASSES - 1:
                return
            if m == 0:
                both_tiles = work.tile([P, TOKEN_TILES, R], F32, tag="low_d_sb")
                low_d_sb[e] = both_tiles
            copy_out(
                OPT["lowd_copy_last"] if e == E - 1 else OPT["lowd_copy"], low_d_sb[e][:, m, :], low_d_banks[(e, m)][:]
            )
            if m == TOKEN_TILES - 1:
                if OPT["s_store"] and e == E - 1:
                    nc.scalar.dma_start(out=out_1[e].rearrange("(p m) r -> p m r", m=TOKEN_TILES), in_=low_d_sb[e][:])
                else:
                    nc.sync.dma_start(out=out_1[e].rearrange("(p m) r -> p m r", m=TOKEN_TILES), in_=low_d_sb[e][:])

        transpose_low()
        transpose_b(0, ("V", "V"))
        lora_product(0, 0, 0)
        lora_product(0, 0, 1)
        lora_out("S", 0, 0, 0)
        lora_out("V", 0, 0, 1)
        transpose_x(0)
        lora_product(0, 0, 2)
        lora_product(0, 0, 3)
        lora_out("V", 0, 0, 2)
        quantise_x(0)
        lora_out("S", 0, 0, 3)
        for q in range(N_BANKS):
            lora_product(0, 1, q)
            lora_out("V" if q % 2 == 0 else "S", 0, 1, q)
        transpose_b(1, OPT["b1_copy"])

        def em(row):
            return row // TOKEN_TILES, row % TOKEN_TILES

        QPOS = OPT["qpos"]
        for row in range(ROWS - 2):
            e, m = em(row)
            gate_up_passes(e, m, 0)
            lora_products(e + 1, m, 0)
            sums(e, m, 0, ("S", e + 1, m, 0))
            if QPOS == 2:
                if row >= 2:
                    quantise_h(*em(row - 2))
                if m == 1:
                    quantise_x(e + 1)
            prod32("G", e, m, 0)
            rnd("G", e, m, 0)
            lora_out("S" if (row >= OPT["ls_from"] or (OPT["ls_odd"] and m == 1)) else "V", e + 1, m, D_PASSES)
            if QPOS == 0:
                if row >= 2:
                    quantise_h(*em(row - 2))
                if m == 1:
                    quantise_x(e + 1)
            gate_up_passes(e, m, 1)
            lora_products(e + 1, m, 1)
            sums(e, m, 1, ("S", e + 1, m, 1))
            lora_out(OPT["l11"], e + 1, m, D_PASSES + 1)
            if QPOS == 1:
                if row >= 2:
                    quantise_h(*em(row - 2))
                if m == 1:
                    quantise_x(e + 1)
            if not OPT["early_b"]:
                prod32("V", e, m, 1)
                rnd("G", e, m, 1)
            if QPOS != 1 and row >= 2:
                low_rank(*em(row - 2))
            if m == 0:
                transpose_x(e + 1)
            if m == 1 and e + 2 < E:
                transpose_b(e + 2, OPT["b_copy"])
            if OPT["early_b"]:
                prod32("G" if row >= OPT["g_from"] else "V", e, m, 1)
                rnd("G", e, m, 1)
            if row >= 1:
                transpose_h(*em(row - 1))
            if QPOS == 1 and row >= 2:
                low_rank(*em(row - 2))

        L = E - 1
        if OPT["endp"] == 2:
            EV = OPT["end"]
            gate_up_passes(L, 0, 0)
            sums(L, 0, 0)
            prod32(EV["m"][0], L, 0, 0)
            quantise_h(L - 1, 0)
            gate_up_passes(L, 0, 1)
            sums(L, 0, 1)
            prod32(EV["m"][1], L, 0, 1)
            rnd(EV["r"][0], L, 0, 0)
            low_rank(L - 1, 0)
            transpose_h(L - 1, 1)
            gate_up_passes(L, 1, 0)
            sums(L, 1, 0)
            prod32(EV["m"][2], L, 1, 0)
            rnd(EV["r"][1], L, 0, 1)
            quantise_h(L - 1, 1)
            gate_up_passes(L, 1, 1)
            sums(L, 1, 1)
            rnd(EV["r"][2], L, 1, 0)
            low_rank(L - 1, 1)
            transpose_h(L, 0)
            transpose_h(L, 1, (0,))
            prod16("V", L, 1, 1)
            prod32(EV["m"][3], L, 1, 1)
            quantise_h(L, 0)
            transpose_h(L, 1, (1,))
            quantise_h(L, 1, (0,))
            low_rank(L, 0)
            low_rank(L, 1, (0,))
            quantise_h(L, 1, (1,))
            low_rank(L, 1, (1,))
        else:
            gate_up_passes(L, 0, 0)
            sums(L, 0, 0)
            prod32("G", L, 0, 0)
            gate_up_passes(L, 0, 1)
            sums(L, 0, 1)
            rnd("S", L, 0, 0)
            quantise_h(L - 1, 0)
            prod32("V", L, 0, 1)
            transpose_h(L - 1, 1)
            low_rank(L - 1, 0)
            gate_up_passes(L, 1, 0)
            sums(L, 1, 0)
            prod32("G", L, 1, 0)
            rnd("S", L, 0, 1)
            gate_up_passes(L, 1, 1)
            sums(L, 1, 1)
            rnd("S", L, 1, 0)
            transpose_h(L, 0)
            transpose_h(L, 1, (0,))
            prod32("V", L, 1, 1)
            rnd("S", L, 1, 1)
            quantise_h(L - 1, 1)
            low_rank(L - 1, 1)
            quantise_h(L, 0)
            transpose_h(L, 1, (1,))
            quantise_h(L, 1, (0,))
            low_rank(L, 0)
            low_rank(L, 1, (0,))
            quantise_h(L, 1, (1,))
            low_rank(L, 1, (1,))
